import numpy as np
import ml_dtypes


def mxq(x, axis, fmt="e4m3"):
    dtype, down = {"e4m3": (ml_dtypes.float8_e4m3fn, 7), "e5m2": (ml_dtypes.float8_e5m2, 14)}[fmt]
    v = np.moveaxis(np.asarray(x, np.float32).astype(ml_dtypes.bfloat16).astype(np.float64), axis, -1)
    blocks = v.reshape(v.shape[:-1] + (-1, 32))
    amax = np.abs(blocks).max(-1, keepdims=True)
    byte = np.maximum(np.where(amax > 0, np.frexp(amax)[1] - 1 + 127, 0) - down, 1)
    scale = np.exp2(byte - 127.0)
    codes = (blocks / scale).astype(np.float32).astype(dtype).astype(np.float64)
    return np.moveaxis((codes * scale).reshape(v.shape), -1, axis)


WIDE = False


def mx_kscale(k):
    if not WIDE:
        return np.ones(k)
    levels = np.array([10, -10, 5, -5, 0])
    a = np.random.permutation(np.resize(levels, k // 512 * 4)).reshape(k // 512, 4)
    idx = np.arange(k)
    return np.exp2(a[idx // 512, idx % 128 // 32])


BF16 = ml_dtypes.bfloat16


def bf(x):
    return np.asarray(x, np.float32).astype(BF16)


def f64(x):
    return np.asarray(x).astype(np.float64)


M, DI, N, DO, TS = 128, 512, 512, 1024, 3
DENSITY = 0.25


def setup_inputs():
    k = mx_kscale(DI)
    m = (np.random.uniform(size=(N, N)) < DENSITY).astype(np.float64)
    return {'x': bf(np.random.standard_normal((M, DI)) * k),
            'W_in': bf(np.random.standard_normal((N, DI)) / np.sqrt(DI) / k),
            'b_in': bf(np.random.standard_normal(N) * 0.3),
            'weights': bf(np.random.standard_normal((N, N)) * 1.5 / np.sqrt(DENSITY * N)),
            'J': bf(np.random.standard_normal((N, N)) * 2.0 / np.sqrt(DENSITY * N)),
            'theta': bf(np.random.uniform(size=N) * 1.0 + 0.25),
            'lam': bf(0.35 + 0.05 * np.random.standard_normal(1)),
            'mask': bf(m * (1.0 - np.eye(N))),
            'noise_raw': bf(np.random.standard_normal((M, N)) * 2.5)}


def reference(x, W_in, b_in, weights, J, theta, lam, mask, noise_raw):
    state = (mxq(f64(x), 1, 'e4m3') @ mxq(f64(W_in), 1, 'e4m3').T) + f64(b_in)
    eff_w = f64(weights) * f64(mask)
    J_m = f64(J) * f64(mask)
    T = np.abs(np.sin(2.0 * f64(theta)))
    signal = mxq(state, 1, 'e4m3') @ mxq(eff_w, 0, 'e4m3')
    s = np.tanh(state)
    delta = (mxq(s, 1, 'e4m3') @ mxq(J_m, 0, 'e4m3')) * s
    noise = f64(noise_raw) * T * 0.1
    return np.tanh(signal + f64(lam) * delta + noise)

@@ -1,0 +1,251 @@
+from contextlib import ExitStack
+import math
+
+import concourse.mybir as mybir
+from concourse.masks import make_identity
+
+F32 = mybir.dt.float32
+BF16 = mybir.dt.bfloat16
+I32 = mybir.dt.int32
+U32 = mybir.dt.uint32
+U8 = mybir.dt.uint8
+FP8X4 = mybir.dt.float8_e4m3fn_x4
+ALU = mybir.AluOpType
+ACT = mybir.ActivationFunctionType
+
+P = 128
+PACK = 4
+M = 128
+DI = 512
+N = 512
+HALF = N // 2
+
+FLOPS = 2 * M * N * (DI + N + N)
+
+HALF_PI_HEAD = 1.5703125
+HALF_PI_TAIL = math.pi / 2 - HALF_PI_HEAD
+
+
+def mask_and_quantise(nc, pool, raw, mask_sb, label):
+    masked = pool.tile([P, PACK, N], BF16, name="masked_" + label)
+    grouped = pool.tile([P, N, PACK], BF16, name="grouped_" + label, align_bytes=64)
+    codes = pool.tile([P, N], U32, name="codes_" + label, align_bytes=64)
+    scales = pool.tile([P, N], U8, name="scales_" + label, align_bytes=64)
+    for h in range(2):
+        cols = slice(h * HALF, (h + 1) * HALF)
+        nc.vector.tensor_tensor(
+            out=masked[:, :, cols], in0=raw[:, :, cols], in1=mask_sb[:, :, cols], op=ALU.mult
+        )
+        side_by_side = grouped[:, cols, :].rearrange("p (c i) t -> p c t i", i=4)
+        row_by_row = masked[:, :, cols].rearrange("p t (c i) -> p c t i", i=4)
+        if h == 0:
+            nc.scalar.copy(out=side_by_side, in_=row_by_row)
+        else:
+            nc.vector.tensor_copy(out=side_by_side, in_=row_by_row)
+    for h in range(2):
+        cols = slice(h * HALF, (h + 1) * HALF)
+        nc.vector.quantize_mx(
+            out=codes[:, cols].bitcast(FP8X4),
+            scales=scales[:, cols],
+            in_=grouped[:, cols, :].rearrange("p n t -> p (n t)"),
+        )
+    return codes, scales
+
+
+def tile_brainquantumlayer_pa_s_kernel(
+    tc, x, W_in, b_in, weights, J, theta, lam, mask, noise_raw, out
+):
+    nc = tc.nc
+    with ExitStack() as ctx:
+        keep = ctx.enter_context(tc.tile_pool(name="keep", bufs=1))
+        turned = ctx.enter_context(tc.psum_pool(name="turned", bufs=4))
+        sums = ctx.enter_context(tc.psum_pool(name="sums", bufs=1))
+
+        theta_sb = keep.tile([P, PACK], BF16)
+        nc.scalar.dma_start(out=theta_sb[:], in_=theta.rearrange("(p t) -> p t", t=PACK))
+        b_sb = keep.tile([P, PACK], BF16)
+        nc.scalar.dma_start(out=b_sb[:], in_=b_in.rearrange("(p t) -> p t", t=PACK))
+        lam_sb = keep.tile([P, 1], BF16)
+        nc.scalar.dma_start(out=lam_sb[:], in_=lam.partition_broadcast(P))
+
+        x_sb = keep.tile([P, DI], BF16)
+        nc.sync.dma_start(out=x_sb[:], in_=x)
+        w_in_sb = keep.tile([P, PACK, DI], BF16)
+        w_in_rows = W_in.rearrange("(p t) k -> p t k", t=PACK)
+        for h in range(2):
+            nc.sync.dma_start(out=w_in_sb[:, 2 * h : 2 * h + 2, :], in_=w_in_rows[:, 2 * h : 2 * h + 2, :])
+        noise_sb = keep.tile([P, N], BF16)
+        nc.sync.dma_start(out=noise_sb[:], in_=noise_raw)
+        mask_sb = keep.tile([P, PACK, N], BF16)
+        nc.sync.dma_start(out=mask_sb[:], in_=mask.rearrange("(p t) n -> p t n", t=PACK))
+        j_sb = keep.tile([P, PACK, N], BF16)
+        nc.sync.dma_start(out=j_sb[:], in_=J.rearrange("(p t) n -> p t n", t=PACK))
+        weights_sb = keep.tile([P, PACK, N], BF16)
+        nc.sync.dma_start(out=weights_sb[:], in_=weights.rearrange("(p t) n -> p t n", t=PACK))
+
+        ident = keep.tile([P, P], F32)
+        make_identity(nc, ident[:])
+
+        b4 = keep.tile([P, PACK], F32)
+        nc.vector.tensor_copy(out=b4[:], in_=b_sb[:])
+        lam_f = keep.tile([P, 1], F32)
+        nc.vector.tensor_copy(out=lam_f[:], in_=lam_sb[:])
+        turns_i = keep.tile([P, PACK], I32)
+        nc.vector.tensor_scalar(out=turns_i[:], in0=theta_sb[:], scalar1=2.0 / math.pi, scalar2=None, op0=ALU.mult)
+        turns = keep.tile([P, PACK], F32)
+        nc.vector.tensor_copy(out=turns[:], in_=turns_i[:])
+        rest_a = keep.tile([P, PACK], F32)
+        nc.vector.scalar_tensor_tensor(
+            out=rest_a[:], in0=turns[:], scalar=-HALF_PI_HEAD, in1=theta_sb[:], op0=ALU.mult, op1=ALU.add
+        )
+        rest = keep.tile([P, PACK], F32)
+        nc.vector.scalar_tensor_tensor(
+            out=rest[:], in0=turns[:], scalar=-HALF_PI_TAIL, in1=rest_a[:], op0=ALU.mult, op1=ALU.add
+        )
+        sine = keep.tile([P, PACK], F32)
+        nc.scalar.activation(out=sine[:], in_=rest[:], func=ACT.Sin, scale=2.0)
+        table_warm = keep.tile([P, PACK], F32)
+        nc.scalar.activation(out=table_warm[:], in_=sine[:], func=ACT.Tanh)
+        t4 = keep.tile([P, PACK], F32)
+        nc.vector.scalar_tensor_tensor(
+            out=t4[:], in0=sine[:], scalar=-1.0, in1=sine[:], op0=ALU.mult, op1=ALU.max
+        )
+
+        x_words = x_sb[:].bitcast(F32)
+        x_turned = turned.tile([P, 2, M], F32, tag="turned")
+        for u in range(2):
+            nc.tensor.transpose(x_turned[:, u, :], x_words[:, u * P : (u + 1) * P], ident[:])
+        x_grouped = keep.tile([P, M, PACK], BF16, align_bytes=64)
+        nc.vector.tensor_copy(out=x_grouped[:].bitcast(F32), in_=x_turned[:].rearrange("q u m -> q m u"))
+
+        w_in_words = w_in_sb[:].bitcast(F32)
+        w_in_grouped = keep.tile([P, PACK, P, PACK], BF16, align_bytes=64)
+        for h in range(2):
+            w_in_turned = turned.tile([P, 2, 2, P], F32, tag="turned")
+            for t in range(2):
+                for u in range(2):
+                    nc.tensor.transpose(
+                        w_in_turned[:, t, u, :], w_in_words[:, 2 * h + t, u * P : (u + 1) * P], ident[:]
+                    )
+            nc.vector.tensor_copy(
+                out=w_in_grouped[:, 2 * h : 2 * h + 2].bitcast(F32),
+                in_=w_in_turned[:].rearrange("q t u j -> q t j u"),
+            )
+
+        x_codes = keep.tile([P, M], U32, align_bytes=64)
+        x_scales = keep.tile([P, M], U8, align_bytes=64)
+        nc.vector.quantize_mx(
+            out=x_codes[:].bitcast(FP8X4), scales=x_scales[:], in_=x_grouped[:].rearrange("q m w -> q (m w)")
+        )
+        w_in_codes = keep.tile([P, N], U32, align_bytes=64)
+        w_in_scales = keep.tile([P, N], U8, align_bytes=64)
+        for h in range(2):
+            cols = slice(h * HALF, (h + 1) * HALF)
+            nc.vector.quantize_mx(
+                out=w_in_codes[:, cols].bitcast(FP8X4),
+                scales=w_in_scales[:, cols],
+                in_=w_in_grouped[:, 2 * h : 2 * h + 2].rearrange("q t j w -> q (t j w)"),
+            )
+
+        t_spread = turned.tile([P, PACK, P], F32, tag="turned")
+        for t in range(PACK):
+            nc.tensor.transpose(t_spread[:, t, :], t4[:, t : t + 1].to_broadcast([P, P]), ident[:])
+        noise_term = keep.tile([P, N], F32)
+        nc.vector.scalar_tensor_tensor(
+            out=noise_term[:].rearrange("m (j t) -> m j t", t=PACK),
+            in0=noise_sb[:].rearrange("m (j t) -> m j t", t=PACK),
+            scalar=0.1,
+            in1=t_spread[:].rearrange("m t j -> m j t"),
+            op0=ALU.mult,
+            op1=ALU.mult,
+        )
+
+        state_for_vector = sums.tile([P, PACK, M], F32)
+        state_for_scalar = sums.tile([P, PACK, M], F32)
+        for bank in (state_for_vector, state_for_scalar):
+            for t in range(PACK):
+                nc.tensor.matmul_mx(
+                    out=bank[:, t, :],
+                    lhsT=w_in_codes[:, t * P : (t + 1) * P].bitcast(FP8X4),
+                    lhsT_scale=w_in_scales[:, t * P : (t + 1) * P],
+                    rhs=x_codes[:].bitcast(FP8X4),
+                    rhs_scale=x_scales[:],
+                    start=True,
+                    stop=True,
+                )
+
+        state_grouped = keep.tile([P, M, PACK], BF16, align_bytes=64)
+        nc.vector.tensor_tensor(
+            out=state_grouped[:],
+            in0=state_for_vector[:].rearrange("j t m -> j m t"),
+            in1=b4[:].unsqueeze(1).to_broadcast([P, M, PACK]),
+            op=ALU.add,
+        )
+        s_turned = keep.tile([P, PACK, M], F32)
+        for t in range(PACK):
+            nc.scalar.activation(
+                out=s_turned[:, t, :], in_=state_for_scalar[:, t, :], func=ACT.Tanh, bias=b4[:, t : t + 1]
+            )
+        s_grouped = keep.tile([P, M, PACK], BF16, align_bytes=64)
+        nc.vector.tensor_copy(out=s_grouped[:], in_=s_turned[:].rearrange("j t m -> j m t"))
+
+        state_codes = keep.tile([P, M], U32, align_bytes=64)
+        state_scales = keep.tile([P, M], U8, align_bytes=64)
+        nc.vector.quantize_mx(
+            out=state_codes[:].bitcast(FP8X4),
+            scales=state_scales[:],
+            in_=state_grouped[:].rearrange("j m t -> j (m t)"),
+        )
+        s_codes = keep.tile([P, M], U32, align_bytes=64)
+        s_scales = keep.tile([P, M], U8, align_bytes=64)
+        nc.vector.quantize_mx(
+            out=s_codes[:].bitcast(FP8X4), scales=s_scales[:], in_=s_grouped[:].rearrange("j m t -> j (m t)")
+        )
+
+        s_back = turned.tile([P, PACK, P], F32, tag="turned")
+        for t in range(PACK):
+            nc.tensor.transpose(s_back[:, t, :], s_turned[:, t, :], ident[:])
+        s_sb = keep.tile([P, N], F32)
+        nc.scalar.copy(
+            out=s_sb[:].rearrange("m (j t) -> m j t", t=PACK), in_=s_back[:].rearrange("m t j -> m j t")
+        )
+
+        j_codes, j_scales = mask_and_quantise(nc, keep, j_sb, mask_sb, "j")
+        w_codes, w_scales = mask_and_quantise(nc, keep, weights_sb, mask_sb, "w")
+
+        delta_ps = sums.tile([P, N], F32)
+        for h in range(2):
+            cols = slice(h * HALF, (h + 1) * HALF)
+            nc.tensor.matmul_mx(
+                out=delta_ps[:, cols],
+                lhsT=s_codes[:].bitcast(FP8X4),
+                lhsT_scale=s_scales[:],
+                rhs=j_codes[:, cols].bitcast(FP8X4),
+                rhs_scale=j_scales[:, cols],
+                start=True,
+                stop=True,
+            )
+        delta = keep.tile([P, N], F32)
+        nc.vector.scalar_tensor_tensor(
+            out=delta[:], in0=delta_ps[:], scalar=lam_f[:, 0:1], in1=s_sb[:], op0=ALU.mult, op1=ALU.mult
+        )
+        rest_of_sum = keep.tile([P, N], F32)
+        nc.vector.tensor_tensor(out=rest_of_sum[:], in0=delta[:], in1=noise_term[:], op=ALU.add)
+
+        signal_ps = sums.tile([P, N], F32)
+        total = keep.tile([P, N], F32)
+        out_sb = keep.tile([P, N], F32)
+        for h in range(2):
+            cols = slice(h * HALF, (h + 1) * HALF)
+            nc.tensor.matmul_mx(
+                out=signal_ps[:, cols],
+                lhsT=state_codes[:].bitcast(FP8X4),
+                lhsT_scale=state_scales[:],
+                rhs=w_codes[:, cols].bitcast(FP8X4),
+                rhs_scale=w_scales[:, cols],
+                start=True,
+                stop=True,
+            )
+            nc.vector.tensor_tensor(out=total[:, cols], in0=signal_ps[:, cols], in1=rest_of_sum[:, cols], op=ALU.add)
+            nc.scalar.activation(out=out_sb[:, cols], in_=total[:, cols], func=ACT.Tanh)
+            nc.sync.dma_start(out=out[:, cols], in_=out_sb[:, cols])

@@ -19,6 +19,7 @@ M = 128
 DI = 512
 N = 512
 HALF = N // 2
+HALVES = (slice(0, HALF), slice(HALF, N))
 
 FLOPS = 2 * M * N * (DI + N + N)
 
@@ -26,30 +27,29 @@ HALF_PI_HEAD = 1.5703125
 HALF_PI_TAIL = math.pi / 2 - HALF_PI_HEAD
 
 
-def mask_and_quantise(nc, pool, raw, mask_sb, label):
-    masked = pool.tile([P, PACK, N], BF16, name="masked_" + label)
-    grouped = pool.tile([P, N, PACK], BF16, name="grouped_" + label, align_bytes=64)
-    codes = pool.tile([P, N], U32, name="codes_" + label, align_bytes=64)
-    scales = pool.tile([P, N], U8, name="scales_" + label, align_bytes=64)
-    for h in range(2):
-        cols = slice(h * HALF, (h + 1) * HALF)
-        nc.vector.tensor_tensor(
-            out=masked[:, :, cols], in0=raw[:, :, cols], in1=mask_sb[:, :, cols], op=ALU.mult
-        )
-        side_by_side = grouped[:, cols, :].rearrange("p (c i) t -> p c t i", i=4)
-        row_by_row = masked[:, :, cols].rearrange("p t (c i) -> p c t i", i=4)
-        if h == 0:
-            nc.scalar.copy(out=side_by_side, in_=row_by_row)
-        else:
-            nc.vector.tensor_copy(out=side_by_side, in_=row_by_row)
-    for h in range(2):
-        cols = slice(h * HALF, (h + 1) * HALF)
-        nc.vector.quantize_mx(
-            out=codes[:, cols].bitcast(FP8X4),
-            scales=scales[:, cols],
-            in_=grouped[:, cols, :].rearrange("p n t -> p (n t)"),
-        )
-    return codes, scales
+def quantise(nc, operand, cols, grouped):
+    nc.vector.quantize_mx(
+        out=operand["codes"][:, cols].bitcast(FP8X4), scales=operand["scales"][:, cols], in_=grouped
+    )
+
+
+def mx_operand(pool, width, label):
+    return {
+        "codes": pool.tile([P, width], U32, name="codes_" + label, align_bytes=64),
+        "scales": pool.tile([P, width], U8, name="scales_" + label, align_bytes=64),
+    }
+
+
+def multiply_mx(nc, acc, stationary, s_cols, moving, m_cols):
+    nc.tensor.matmul_mx(
+        out=acc,
+        lhsT=stationary["codes"][:, s_cols].bitcast(FP8X4),
+        lhsT_scale=stationary["scales"][:, s_cols],
+        rhs=moving["codes"][:, m_cols].bitcast(FP8X4),
+        rhs_scale=moving["scales"][:, m_cols],
+        start=True,
+        stop=True,
+    )
 
 
 def tile_brainquantumlayer_pa_s_kernel(
@@ -60,6 +60,7 @@ def tile_brainquantumlayer_pa_s_kernel(
         keep = ctx.enter_context(tc.tile_pool(name="keep", bufs=1))
         turned = ctx.enter_context(tc.psum_pool(name="turned", bufs=4))
         sums = ctx.enter_context(tc.psum_pool(name="sums", bufs=1))
+        ctx.enter_context(tc.manual_schedule())
 
         theta_sb = keep.tile([P, PACK], BF16)
         nc.scalar.dma_start(out=theta_sb[:], in_=theta.rearrange("(p t) -> p t", t=PACK))
@@ -86,10 +87,6 @@ def tile_brainquantumlayer_pa_s_kernel(
         ident = keep.tile([P, P], F32)
         make_identity(nc, ident[:])
 
-        b4 = keep.tile([P, PACK], F32)
-        nc.vector.tensor_copy(out=b4[:], in_=b_sb[:])
-        lam_f = keep.tile([P, 1], F32)
-        nc.vector.tensor_copy(out=lam_f[:], in_=lam_sb[:])
         turns_i = keep.tile([P, PACK], I32)
         nc.vector.tensor_scalar(out=turns_i[:], in0=theta_sb[:], scalar1=2.0 / math.pi, scalar2=None, op0=ALU.mult)
         turns = keep.tile([P, PACK], F32)
@@ -106,10 +103,10 @@ def tile_brainquantumlayer_pa_s_kernel(
         nc.scalar.activation(out=sine[:], in_=rest[:], func=ACT.Sin, scale=2.0)
         table_warm = keep.tile([P, PACK], F32)
         nc.scalar.activation(out=table_warm[:], in_=sine[:], func=ACT.Tanh)
-        t4 = keep.tile([P, PACK], F32)
-        nc.vector.scalar_tensor_tensor(
-            out=t4[:], in0=sine[:], scalar=-1.0, in1=sine[:], op0=ALU.mult, op1=ALU.max
-        )
+        b4 = keep.tile([P, PACK], F32)
+        nc.vector.tensor_copy(out=b4[:], in_=b_sb[:])
+        lam_f = keep.tile([P, 1], F32)
+        nc.vector.tensor_copy(out=lam_f[:], in_=lam_sb[:])
 
         x_words = x_sb[:].bitcast(F32)
         x_turned = turned.tile([P, 2, M], F32, tag="turned")
@@ -117,9 +114,15 @@ def tile_brainquantumlayer_pa_s_kernel(
             nc.tensor.transpose(x_turned[:, u, :], x_words[:, u * P : (u + 1) * P], ident[:])
         x_grouped = keep.tile([P, M, PACK], BF16, align_bytes=64)
         nc.vector.tensor_copy(out=x_grouped[:].bitcast(F32), in_=x_turned[:].rearrange("q u m -> q m u"))
+        t4 = keep.tile([P, PACK], F32)
+        nc.vector.scalar_tensor_tensor(
+            out=t4[:], in0=sine[:], scalar=-1.0, in1=sine[:], op0=ALU.mult, op1=ALU.max
+        )
 
         w_in_words = w_in_sb[:].bitcast(F32)
         w_in_grouped = keep.tile([P, PACK, P, PACK], BF16, align_bytes=64)
+        x_mx = mx_operand(keep, M, "x")
+        w_in_mx = mx_operand(keep, N, "w_in")
         for h in range(2):
             w_in_turned = turned.tile([P, 2, 2, P], F32, tag="turned")
             for t in range(2):
@@ -127,29 +130,18 @@ def tile_brainquantumlayer_pa_s_kernel(
                     nc.tensor.transpose(
                         w_in_turned[:, t, u, :], w_in_words[:, 2 * h + t, u * P : (u + 1) * P], ident[:]
                     )
-            nc.vector.tensor_copy(
+            empty = nc.vector.tensor_copy if h == 0 else nc.scalar.copy
+            empty(
                 out=w_in_grouped[:, 2 * h : 2 * h + 2].bitcast(F32),
                 in_=w_in_turned[:].rearrange("q t u j -> q t j u"),
             )
-
-        x_codes = keep.tile([P, M], U32, align_bytes=64)
-        x_scales = keep.tile([P, M], U8, align_bytes=64)
-        nc.vector.quantize_mx(
-            out=x_codes[:].bitcast(FP8X4), scales=x_scales[:], in_=x_grouped[:].rearrange("q m w -> q (m w)")
-        )
-        w_in_codes = keep.tile([P, N], U32, align_bytes=64)
-        w_in_scales = keep.tile([P, N], U8, align_bytes=64)
-        for h in range(2):
-            cols = slice(h * HALF, (h + 1) * HALF)
-            nc.vector.quantize_mx(
-                out=w_in_codes[:, cols].bitcast(FP8X4),
-                scales=w_in_scales[:, cols],
-                in_=w_in_grouped[:, 2 * h : 2 * h + 2].rearrange("q t j w -> q (t j w)"),
-            )
+            if h == 0:
+                quantise(nc, x_mx, slice(0, M), x_grouped[:].rearrange("q m w -> q (m w)"))
 
         t_spread = turned.tile([P, PACK, P], F32, tag="turned")
         for t in range(PACK):
             nc.tensor.transpose(t_spread[:, t, :], t4[:, t : t + 1].to_broadcast([P, P]), ident[:])
+        quantise(nc, w_in_mx, HALVES[0], w_in_grouped[:, 0:2].rearrange("q t j w -> q (t j w)"))
         noise_term = keep.tile([P, N], F32)
         nc.vector.scalar_tensor_tensor(
             out=noise_term[:].rearrange("m (j t) -> m j t", t=PACK),
@@ -159,93 +151,90 @@ def tile_brainquantumlayer_pa_s_kernel(
             op0=ALU.mult,
             op1=ALU.mult,
         )
+        quantise(nc, w_in_mx, HALVES[1], w_in_grouped[:, 2:4].rearrange("q t j w -> q (t j w)"))
 
-        state_for_vector = sums.tile([P, PACK, M], F32)
-        state_for_scalar = sums.tile([P, PACK, M], F32)
-        for bank in (state_for_vector, state_for_scalar):
-            for t in range(PACK):
-                nc.tensor.matmul_mx(
-                    out=bank[:, t, :],
-                    lhsT=w_in_codes[:, t * P : (t + 1) * P].bitcast(FP8X4),
-                    lhsT_scale=w_in_scales[:, t * P : (t + 1) * P],
-                    rhs=x_codes[:].bitcast(FP8X4),
-                    rhs_scale=x_scales[:],
-                    start=True,
-                    stop=True,
-                )
-
-        state_grouped = keep.tile([P, M, PACK], BF16, align_bytes=64)
+        state_ps = sums.tile([P, PACK, M], F32)
+        for t in range(PACK):
+            multiply_mx(nc, state_ps[:, t, :], w_in_mx, slice(t * P, (t + 1) * P), x_mx, slice(0, M))
+        state_f = keep.tile([P, M, PACK], F32)
         nc.vector.tensor_tensor(
-            out=state_grouped[:],
-            in0=state_for_vector[:].rearrange("j t m -> j m t"),
+            out=state_f[:],
+            in0=state_ps[:].rearrange("j t m -> j m t"),
             in1=b4[:].unsqueeze(1).to_broadcast([P, M, PACK]),
             op=ALU.add,
         )
-        s_turned = keep.tile([P, PACK, M], F32)
-        for t in range(PACK):
-            nc.scalar.activation(
-                out=s_turned[:, t, :], in_=state_for_scalar[:, t, :], func=ACT.Tanh, bias=b4[:, t : t + 1]
-            )
         s_grouped = keep.tile([P, M, PACK], BF16, align_bytes=64)
-        nc.vector.tensor_copy(out=s_grouped[:], in_=s_turned[:].rearrange("j t m -> j m t"))
+        nc.scalar.activation(out=s_grouped[:], in_=state_f[:], func=ACT.Tanh)
+        s_turned = keep.tile([P, PACK, M], F32)
+        nc.scalar.activation(out=s_turned[:], in_=state_f[:].rearrange("j m t -> j t m"), func=ACT.Tanh)
 
-        state_codes = keep.tile([P, M], U32, align_bytes=64)
-        state_scales = keep.tile([P, M], U8, align_bytes=64)
-        nc.vector.quantize_mx(
-            out=state_codes[:].bitcast(FP8X4),
-            scales=state_scales[:],
-            in_=state_grouped[:].rearrange("j m t -> j (m t)"),
-        )
-        s_codes = keep.tile([P, M], U32, align_bytes=64)
-        s_scales = keep.tile([P, M], U8, align_bytes=64)
-        nc.vector.quantize_mx(
-            out=s_codes[:].bitcast(FP8X4), scales=s_scales[:], in_=s_grouped[:].rearrange("j m t -> j (m t)")
-        )
+        raw = {"j": j_sb, "w": weights_sb}
+        masked = {}
+        grouped = {}
+        mx = {}
+        for label in ("j", "w"):
+            masked[label] = keep.tile([P, PACK, N], BF16, name="masked_" + label)
+            grouped[label] = keep.tile([P, N, PACK], BF16, name="grouped_" + label, align_bytes=64)
+            mx[label] = mx_operand(keep, N, label)
 
+        def apply_mask(label, h):
+            cols = HALVES[h]
+            nc.vector.tensor_tensor(
+                out=masked[label][:, :, cols], in0=raw[label][:, :, cols], in1=mask_sb[:, :, cols], op=ALU.mult
+            )
+
+        def regroup(copy, label, h):
+            cols = HALVES[h]
+            copy(
+                out=grouped[label][:, cols, :].rearrange("p (c i) t -> p c t i", i=4),
+                in_=masked[label][:, :, cols].rearrange("p t (c i) -> p c t i", i=4),
+            )
+
+        def quantise_masked(label, h):
+            cols = HALVES[h]
+            quantise(nc, mx[label], cols, grouped[label][:, cols, :].rearrange("p n t -> p (n t)"))
+
+        s_mx = mx_operand(keep, M, "s")
+        state_mx = mx_operand(keep, M, "state")
+        delta_ps = sums.tile([P, N], F32)
+        signal_ps = sums.tile([P, N], F32)
+
+        apply_mask("j", 0)
+        regroup(nc.scalar.copy, "j", 0)
+        apply_mask("j", 1)
+        quantise(nc, s_mx, slice(0, M), s_grouped[:].rearrange("j m t -> j (m t)"))
         s_back = turned.tile([P, PACK, P], F32, tag="turned")
         for t in range(PACK):
             nc.tensor.transpose(s_back[:, t, :], s_turned[:, t, :], ident[:])
+        regroup(nc.vector.tensor_copy, "j", 1)
         s_sb = keep.tile([P, N], F32)
         nc.scalar.copy(
             out=s_sb[:].rearrange("m (j t) -> m j t", t=PACK), in_=s_back[:].rearrange("m t j -> m j t")
         )
-
-        j_codes, j_scales = mask_and_quantise(nc, keep, j_sb, mask_sb, "j")
-        w_codes, w_scales = mask_and_quantise(nc, keep, weights_sb, mask_sb, "w")
-
-        delta_ps = sums.tile([P, N], F32)
+        apply_mask("w", 0)
+        regroup(nc.scalar.copy, "w", 0)
+        apply_mask("w", 1)
+        state_grouped = keep.tile([P, M, PACK], BF16, align_bytes=64)
+        nc.scalar.copy(out=state_grouped[:], in_=state_f[:])
         for h in range(2):
-            cols = slice(h * HALF, (h + 1) * HALF)
-            nc.tensor.matmul_mx(
-                out=delta_ps[:, cols],
-                lhsT=s_codes[:].bitcast(FP8X4),
-                lhsT_scale=s_scales[:],
-                rhs=j_codes[:, cols].bitcast(FP8X4),
-                rhs_scale=j_scales[:, cols],
-                start=True,
-                stop=True,
-            )
+            quantise_masked("j", h)
+            multiply_mx(nc, delta_ps[:, HALVES[h]], s_mx, slice(0, M), mx["j"], HALVES[h])
+        regroup(nc.vector.tensor_copy, "w", 1)
         delta = keep.tile([P, N], F32)
         nc.vector.scalar_tensor_tensor(
             out=delta[:], in0=delta_ps[:], scalar=lam_f[:, 0:1], in1=s_sb[:], op0=ALU.mult, op1=ALU.mult
         )
+        quantise_masked("w", 0)
+        quantise(nc, state_mx, slice(0, M), state_grouped[:].rearrange("j m t -> j (m t)"))
+        multiply_mx(nc, signal_ps[:, HALVES[0]], state_mx, slice(0, M), mx["w"], HALVES[0])
+        quantise_masked("w", 1)
+        multiply_mx(nc, signal_ps[:, HALVES[1]], state_mx, slice(0, M), mx["w"], HALVES[1])
         rest_of_sum = keep.tile([P, N], F32)
         nc.vector.tensor_tensor(out=rest_of_sum[:], in0=delta[:], in1=noise_term[:], op=ALU.add)
 
-        signal_ps = sums.tile([P, N], F32)
         total = keep.tile([P, N], F32)
         out_sb = keep.tile([P, N], F32)
-        for h in range(2):
-            cols = slice(h * HALF, (h + 1) * HALF)
-            nc.tensor.matmul_mx(
-                out=signal_ps[:, cols],
-                lhsT=state_codes[:].bitcast(FP8X4),
-                lhsT_scale=state_scales[:],
-                rhs=w_codes[:, cols].bitcast(FP8X4),
-                rhs_scale=w_scales[:, cols],
-                start=True,
-                stop=True,
-            )
+        for cols in HALVES:
             nc.vector.tensor_tensor(out=total[:, cols], in0=signal_ps[:, cols], in1=rest_of_sum[:, cols], op=ALU.add)
             nc.scalar.activation(out=out_sb[:, cols], in_=total[:, cols], func=ACT.Tanh)
             nc.sync.dma_start(out=out[:, cols], in_=out_sb[:, cols])

@@ -58,7 +58,7 @@ def tile_brainquantumlayer_pa_s_kernel(
     nc = tc.nc
     with ExitStack() as ctx:
         keep = ctx.enter_context(tc.tile_pool(name="keep", bufs=1))
-        turned = ctx.enter_context(tc.psum_pool(name="turned", bufs=4))
+        turned = ctx.enter_context(tc.psum_pool(name="turned", bufs=5))
         sums = ctx.enter_context(tc.psum_pool(name="sums", bufs=1))
         ctx.enter_context(tc.manual_schedule())
 
@@ -73,8 +73,8 @@ def tile_brainquantumlayer_pa_s_kernel(
         nc.sync.dma_start(out=x_sb[:], in_=x)
         w_in_sb = keep.tile([P, PACK, DI], BF16)
         w_in_rows = W_in.rearrange("(p t) k -> p t k", t=PACK)
-        for h in range(2):
-            nc.sync.dma_start(out=w_in_sb[:, 2 * h : 2 * h + 2, :], in_=w_in_rows[:, 2 * h : 2 * h + 2, :])
+        for t in range(PACK):
+            nc.sync.dma_start(out=w_in_sb[:, t, :], in_=w_in_rows[:, t, :])
         noise_sb = keep.tile([P, N], BF16)
         nc.sync.dma_start(out=noise_sb[:], in_=noise_raw)
         mask_sb = keep.tile([P, PACK, N], BF16)
@@ -86,6 +86,11 @@ def tile_brainquantumlayer_pa_s_kernel(
 
         ident = keep.tile([P, P], F32)
         make_identity(nc, ident[:])
+
+        zero = keep.tile([P, 1], F32)
+        nc.vector.memset(zero[:], 0.0)
+        table_warm = keep.tile([P, 1], F32)
+        nc.scalar.activation(out=table_warm[:], in_=zero[:], func=ACT.Silu)
 
         turns_i = keep.tile([P, PACK], I32)
         nc.vector.tensor_scalar(out=turns_i[:], in0=theta_sb[:], scalar1=2.0 / math.pi, scalar2=None, op0=ALU.mult)
@@ -101,13 +106,13 @@ def tile_brainquantumlayer_pa_s_kernel(
         )
         sine = keep.tile([P, PACK], F32)
         nc.scalar.activation(out=sine[:], in_=rest[:], func=ACT.Sin, scale=2.0)
-        table_warm = keep.tile([P, PACK], F32)
-        nc.scalar.activation(out=table_warm[:], in_=sine[:], func=ACT.Tanh)
         b4 = keep.tile([P, PACK], F32)
         nc.vector.tensor_copy(out=b4[:], in_=b_sb[:])
         lam_f = keep.tile([P, 1], F32)
         nc.vector.tensor_copy(out=lam_f[:], in_=lam_sb[:])
 
+        x_mx = mx_operand(keep, M, "x")
+        w_in_mx = mx_operand(keep, N, "w_in")
         x_words = x_sb[:].bitcast(F32)
         x_turned = turned.tile([P, 2, M], F32, tag="turned")
         for u in range(2):
@@ -121,27 +126,26 @@ def tile_brainquantumlayer_pa_s_kernel(
 
         w_in_words = w_in_sb[:].bitcast(F32)
         w_in_grouped = keep.tile([P, PACK, P, PACK], BF16, align_bytes=64)
-        x_mx = mx_operand(keep, M, "x")
-        w_in_mx = mx_operand(keep, N, "w_in")
-        for h in range(2):
-            w_in_turned = turned.tile([P, 2, 2, P], F32, tag="turned")
-            for t in range(2):
-                for u in range(2):
-                    nc.tensor.transpose(
-                        w_in_turned[:, t, u, :], w_in_words[:, 2 * h + t, u * P : (u + 1) * P], ident[:]
-                    )
-            empty = nc.vector.tensor_copy if h == 0 else nc.scalar.copy
-            empty(
-                out=w_in_grouped[:, 2 * h : 2 * h + 2].bitcast(F32),
-                in_=w_in_turned[:].rearrange("q t u j -> q t j u"),
-            )
-            if h == 0:
+        for t in range(PACK):
+            w_in_turned = turned.tile([P, 2, P], F32, tag="turned")
+            for u in range(2):
+                nc.tensor.transpose(w_in_turned[:, u, :], w_in_words[:, t, u * P : (u + 1) * P], ident[:])
+            empty = nc.scalar.copy if t % 2 == 0 else nc.vector.tensor_copy
+            empty(out=w_in_grouped[:, t].bitcast(F32), in_=w_in_turned[:].rearrange("q u j -> q j u"))
+            if t == 0:
                 quantise(nc, x_mx, slice(0, M), x_grouped[:].rearrange("q m w -> q (m w)"))
-
+            else:
+                quantise(
+                    nc, w_in_mx, slice((t - 1) * P, t * P), w_in_grouped[:, t - 1].rearrange("q j w -> q (j w)")
+                )
         t_spread = turned.tile([P, PACK, P], F32, tag="turned")
         for t in range(PACK):
             nc.tensor.transpose(t_spread[:, t, :], t4[:, t : t + 1].to_broadcast([P, P]), ident[:])
-        quantise(nc, w_in_mx, HALVES[0], w_in_grouped[:, 0:2].rearrange("q t j w -> q (t j w)"))
+        quantise(nc, w_in_mx, slice(3 * P, 4 * P), w_in_grouped[:, 3].rearrange("q j w -> q (j w)"))
+
+        state_ps = sums.tile([P, PACK, M], F32)
+        for t in range(PACK):
+            multiply_mx(nc, state_ps[:, t, :], w_in_mx, slice(t * P, (t + 1) * P), x_mx, slice(0, M))
         noise_term = keep.tile([P, N], F32)
         nc.vector.scalar_tensor_tensor(
             out=noise_term[:].rearrange("m (j t) -> m j t", t=PACK),
@@ -151,11 +155,6 @@ def tile_brainquantumlayer_pa_s_kernel(
             op0=ALU.mult,
             op1=ALU.mult,
         )
-        quantise(nc, w_in_mx, HALVES[1], w_in_grouped[:, 2:4].rearrange("q t j w -> q (t j w)"))
-
-        state_ps = sums.tile([P, PACK, M], F32)
-        for t in range(PACK):
-            multiply_mx(nc, state_ps[:, t, :], w_in_mx, slice(t * P, (t + 1) * P), x_mx, slice(0, M))
         state_f = keep.tile([P, M, PACK], F32)
         nc.vector.tensor_tensor(
             out=state_f[:],
@@ -199,42 +198,41 @@ def tile_brainquantumlayer_pa_s_kernel(
         delta_ps = sums.tile([P, N], F32)
         signal_ps = sums.tile([P, N], F32)
 
-        apply_mask("j", 0)
-        regroup(nc.scalar.copy, "j", 0)
-        apply_mask("j", 1)
+        for h in range(2):
+            apply_mask("j", h)
+            regroup(nc.scalar.copy, "j", h)
         quantise(nc, s_mx, slice(0, M), s_grouped[:].rearrange("j m t -> j (m t)"))
         s_back = turned.tile([P, PACK, P], F32, tag="turned")
         for t in range(PACK):
             nc.tensor.transpose(s_back[:, t, :], s_turned[:, t, :], ident[:])
-        regroup(nc.vector.tensor_copy, "j", 1)
         s_sb = keep.tile([P, N], F32)
         nc.scalar.copy(
             out=s_sb[:].rearrange("m (j t) -> m j t", t=PACK), in_=s_back[:].rearrange("m t j -> m j t")
         )
+        state_grouped = keep.tile([P, M, PACK], BF16, align_bytes=64)
+        nc.scalar.copy(out=state_grouped[:], in_=state_f[:])
         apply_mask("w", 0)
         regroup(nc.scalar.copy, "w", 0)
         apply_mask("w", 1)
-        state_grouped = keep.tile([P, M, PACK], BF16, align_bytes=64)
-        nc.scalar.copy(out=state_grouped[:], in_=state_f[:])
+        regroup(nc.vector.tensor_copy, "w", 1)
         for h in range(2):
             quantise_masked("j", h)
             multiply_mx(nc, delta_ps[:, HALVES[h]], s_mx, slice(0, M), mx["j"], HALVES[h])
-        regroup(nc.vector.tensor_copy, "w", 1)
+        quantise_masked("w", 1)
+        quantise(nc, state_mx, slice(0, M), state_grouped[:].rearrange("j m t -> j (m t)"))
+        multiply_mx(nc, signal_ps[:, HALVES[1]], state_mx, slice(0, M), mx["w"], HALVES[1])
         delta = keep.tile([P, N], F32)
         nc.vector.scalar_tensor_tensor(
             out=delta[:], in0=delta_ps[:], scalar=lam_f[:, 0:1], in1=s_sb[:], op0=ALU.mult, op1=ALU.mult
         )
         quantise_masked("w", 0)
-        quantise(nc, state_mx, slice(0, M), state_grouped[:].rearrange("j m t -> j (m t)"))
         multiply_mx(nc, signal_ps[:, HALVES[0]], state_mx, slice(0, M), mx["w"], HALVES[0])
-        quantise_masked("w", 1)
-        multiply_mx(nc, signal_ps[:, HALVES[1]], state_mx, slice(0, M), mx["w"], HALVES[1])
         rest_of_sum = keep.tile([P, N], F32)
         nc.vector.tensor_tensor(out=rest_of_sum[:], in0=delta[:], in1=noise_term[:], op=ALU.add)
 
         total = keep.tile([P, N], F32)
         out_sb = keep.tile([P, N], F32)
-        for cols in HALVES:
+        for cols in reversed(HALVES):
             nc.vector.tensor_tensor(out=total[:, cols], in0=signal_ps[:, cols], in1=rest_of_sum[:, cols], op=ALU.add)
             nc.scalar.activation(out=out_sb[:, cols], in_=total[:, cols], func=ACT.Tanh)
             nc.sync.dma_start(out=out[:, cols], in_=out_sb[:, cols])

@@ -73,8 +73,8 @@ def tile_brainquantumlayer_pa_s_kernel(
         nc.sync.dma_start(out=x_sb[:], in_=x)
         w_in_sb = keep.tile([P, PACK, DI], BF16)
         w_in_rows = W_in.rearrange("(p t) k -> p t k", t=PACK)
-        for t in range(PACK):
-            nc.sync.dma_start(out=w_in_sb[:, t, :], in_=w_in_rows[:, t, :])
+        for rows in (slice(0, 2), slice(2, PACK)):
+            nc.sync.dma_start(out=w_in_sb[:, rows, :], in_=w_in_rows[:, rows, :])
         noise_sb = keep.tile([P, N], BF16)
         nc.sync.dma_start(out=noise_sb[:], in_=noise_raw)
         mask_sb = keep.tile([P, PACK, N], BF16)
@@ -106,10 +106,8 @@ def tile_brainquantumlayer_pa_s_kernel(
         )
         sine = keep.tile([P, PACK], F32)
         nc.scalar.activation(out=sine[:], in_=rest[:], func=ACT.Sin, scale=2.0)
-        b4 = keep.tile([P, PACK], F32)
-        nc.vector.tensor_copy(out=b4[:], in_=b_sb[:])
-        lam_f = keep.tile([P, 1], F32)
-        nc.vector.tensor_copy(out=lam_f[:], in_=lam_sb[:])
+        t4 = keep.tile([P, PACK], F32)
+        nc.scalar.activation(out=t4[:], in_=sine[:], func=ACT.Abs, scale=0.1)
 
         x_mx = mx_operand(keep, M, "x")
         w_in_mx = mx_operand(keep, N, "w_in")
@@ -119,10 +117,6 @@ def tile_brainquantumlayer_pa_s_kernel(
             nc.tensor.transpose(x_turned[:, u, :], x_words[:, u * P : (u + 1) * P], ident[:])
         x_grouped = keep.tile([P, M, PACK], BF16, align_bytes=64)
         nc.vector.tensor_copy(out=x_grouped[:].bitcast(F32), in_=x_turned[:].rearrange("q u m -> q m u"))
-        t4 = keep.tile([P, PACK], F32)
-        nc.vector.scalar_tensor_tensor(
-            out=t4[:], in0=sine[:], scalar=-1.0, in1=sine[:], op0=ALU.mult, op1=ALU.max
-        )
 
         w_in_words = w_in_sb[:].bitcast(F32)
         w_in_grouped = keep.tile([P, PACK, P, PACK], BF16, align_bytes=64)
@@ -147,19 +141,17 @@ def tile_brainquantumlayer_pa_s_kernel(
         for t in range(PACK):
             multiply_mx(nc, state_ps[:, t, :], w_in_mx, slice(t * P, (t + 1) * P), x_mx, slice(0, M))
         noise_term = keep.tile([P, N], F32)
-        nc.vector.scalar_tensor_tensor(
+        nc.vector.tensor_tensor(
             out=noise_term[:].rearrange("m (j t) -> m j t", t=PACK),
             in0=noise_sb[:].rearrange("m (j t) -> m j t", t=PACK),
-            scalar=0.1,
             in1=t_spread[:].rearrange("m t j -> m j t"),
-            op0=ALU.mult,
-            op1=ALU.mult,
+            op=ALU.mult,
         )
         state_f = keep.tile([P, M, PACK], F32)
         nc.vector.tensor_tensor(
             out=state_f[:],
             in0=state_ps[:].rearrange("j t m -> j m t"),
-            in1=b4[:].unsqueeze(1).to_broadcast([P, M, PACK]),
+            in1=b_sb[:].unsqueeze(1).to_broadcast([P, M, PACK]),
             op=ALU.add,
         )
         s_grouped = keep.tile([P, M, PACK], BF16, align_bytes=64)
@@ -198,41 +190,42 @@ def tile_brainquantumlayer_pa_s_kernel(
         delta_ps = sums.tile([P, N], F32)
         signal_ps = sums.tile([P, N], F32)
 
-        for h in range(2):
-            apply_mask("j", h)
-            regroup(nc.scalar.copy, "j", h)
+        apply_mask("j", 0)
+        regroup(nc.scalar.copy, "j", 0)
+        apply_mask("j", 1)
         quantise(nc, s_mx, slice(0, M), s_grouped[:].rearrange("j m t -> j (m t)"))
         s_back = turned.tile([P, PACK, P], F32, tag="turned")
         for t in range(PACK):
             nc.tensor.transpose(s_back[:, t, :], s_turned[:, t, :], ident[:])
+        regroup(nc.vector.tensor_copy, "j", 1)
         s_sb = keep.tile([P, N], F32)
         nc.scalar.copy(
             out=s_sb[:].rearrange("m (j t) -> m j t", t=PACK), in_=s_back[:].rearrange("m t j -> m j t")
         )
-        state_grouped = keep.tile([P, M, PACK], BF16, align_bytes=64)
-        nc.scalar.copy(out=state_grouped[:], in_=state_f[:])
         apply_mask("w", 0)
         regroup(nc.scalar.copy, "w", 0)
         apply_mask("w", 1)
-        regroup(nc.vector.tensor_copy, "w", 1)
+        state_grouped = keep.tile([P, M, PACK], BF16, align_bytes=64)
+        nc.scalar.copy(out=state_grouped[:], in_=state_f[:])
         for h in range(2):
             quantise_masked("j", h)
             multiply_mx(nc, delta_ps[:, HALVES[h]], s_mx, slice(0, M), mx["j"], HALVES[h])
-        quantise_masked("w", 1)
-        quantise(nc, state_mx, slice(0, M), state_grouped[:].rearrange("j m t -> j (m t)"))
-        multiply_mx(nc, signal_ps[:, HALVES[1]], state_mx, slice(0, M), mx["w"], HALVES[1])
+        regroup(nc.vector.tensor_copy, "w", 1)
         delta = keep.tile([P, N], F32)
         nc.vector.scalar_tensor_tensor(
-            out=delta[:], in0=delta_ps[:], scalar=lam_f[:, 0:1], in1=s_sb[:], op0=ALU.mult, op1=ALU.mult
+            out=delta[:], in0=delta_ps[:], scalar=lam_sb[:, 0:1], in1=s_sb[:], op0=ALU.mult, op1=ALU.mult
         )
         quantise_masked("w", 0)
+        quantise(nc, state_mx, slice(0, M), state_grouped[:].rearrange("j m t -> j (m t)"))
         multiply_mx(nc, signal_ps[:, HALVES[0]], state_mx, slice(0, M), mx["w"], HALVES[0])
+        quantise_masked("w", 1)
+        multiply_mx(nc, signal_ps[:, HALVES[1]], state_mx, slice(0, M), mx["w"], HALVES[1])
         rest_of_sum = keep.tile([P, N], F32)
         nc.vector.tensor_tensor(out=rest_of_sum[:], in0=delta[:], in1=noise_term[:], op=ALU.add)
 
         total = keep.tile([P, N], F32)
         out_sb = keep.tile([P, N], F32)
-        for cols in reversed(HALVES):
+        for cols in HALVES:
             nc.vector.tensor_tensor(out=total[:, cols], in0=signal_ps[:, cols], in1=rest_of_sum[:, cols], op=ALU.add)
             nc.scalar.activation(out=out_sb[:, cols], in_=total[:, cols], func=ACT.Tanh)
             nc.sync.dma_start(out=out[:, cols], in_=out_sb[:, cols])

@@ -20,6 +20,7 @@ DI = 512
 N = 512
 HALF = N // 2
 HALVES = (slice(0, HALF), slice(HALF, N))
+ROW_HALVES = (slice(0, 2), slice(2, PACK))
 
 FLOPS = 2 * M * N * (DI + N + N)
 
@@ -73,16 +74,19 @@ def tile_brainquantumlayer_pa_s_kernel(
         nc.sync.dma_start(out=x_sb[:], in_=x)
         w_in_sb = keep.tile([P, PACK, DI], BF16)
         w_in_rows = W_in.rearrange("(p t) k -> p t k", t=PACK)
-        for rows in (slice(0, 2), slice(2, PACK)):
+        for rows in ROW_HALVES:
             nc.sync.dma_start(out=w_in_sb[:, rows, :], in_=w_in_rows[:, rows, :])
-        noise_sb = keep.tile([P, N], BF16)
-        nc.sync.dma_start(out=noise_sb[:], in_=noise_raw)
         mask_sb = keep.tile([P, PACK, N], BF16)
-        nc.sync.dma_start(out=mask_sb[:], in_=mask.rearrange("(p t) n -> p t n", t=PACK))
+        mask_rows = mask.rearrange("(p t) n -> p t n", t=PACK)
         j_sb = keep.tile([P, PACK, N], BF16)
-        nc.sync.dma_start(out=j_sb[:], in_=J.rearrange("(p t) n -> p t n", t=PACK))
+        j_rows = J.rearrange("(p t) n -> p t n", t=PACK)
+        for rows in ROW_HALVES:
+            nc.sync.dma_start(out=mask_sb[:, rows, :], in_=mask_rows[:, rows, :])
+            nc.sync.dma_start(out=j_sb[:, rows, :], in_=j_rows[:, rows, :])
         weights_sb = keep.tile([P, PACK, N], BF16)
         nc.sync.dma_start(out=weights_sb[:], in_=weights.rearrange("(p t) n -> p t n", t=PACK))
+        noise_sb = keep.tile([P, N], BF16)
+        nc.sync.dma_start(out=noise_sb[:], in_=noise_raw)
 
         ident = keep.tile([P, P], F32)
         make_identity(nc, ident[:])
@@ -91,6 +95,15 @@ def tile_brainquantumlayer_pa_s_kernel(
         nc.vector.memset(zero[:], 0.0)
         table_warm = keep.tile([P, 1], F32)
         nc.scalar.activation(out=table_warm[:], in_=zero[:], func=ACT.Silu)
+
+        x_mx = mx_operand(keep, M, "x")
+        w_in_mx = mx_operand(keep, N, "w_in")
+        x_words = x_sb[:].bitcast(F32)
+        x_turned = turned.tile([P, 2, M], F32, tag="turned")
+        for u in range(2):
+            nc.tensor.transpose(x_turned[:, u, :], x_words[:, u * P : (u + 1) * P], ident[:])
+        x_grouped = keep.tile([P, M, PACK], BF16, align_bytes=64)
+        nc.vector.tensor_copy(out=x_grouped[:].bitcast(F32), in_=x_turned[:].rearrange("q u m -> q m u"))
 
         turns_i = keep.tile([P, PACK], I32)
         nc.vector.tensor_scalar(out=turns_i[:], in0=theta_sb[:], scalar1=2.0 / math.pi, scalar2=None, op0=ALU.mult)
@@ -104,19 +117,6 @@ def tile_brainquantumlayer_pa_s_kernel(
         nc.vector.scalar_tensor_tensor(
             out=rest[:], in0=turns[:], scalar=-HALF_PI_TAIL, in1=rest_a[:], op0=ALU.mult, op1=ALU.add
         )
-        sine = keep.tile([P, PACK], F32)
-        nc.scalar.activation(out=sine[:], in_=rest[:], func=ACT.Sin, scale=2.0)
-        t4 = keep.tile([P, PACK], F32)
-        nc.scalar.activation(out=t4[:], in_=sine[:], func=ACT.Abs, scale=0.1)
-
-        x_mx = mx_operand(keep, M, "x")
-        w_in_mx = mx_operand(keep, N, "w_in")
-        x_words = x_sb[:].bitcast(F32)
-        x_turned = turned.tile([P, 2, M], F32, tag="turned")
-        for u in range(2):
-            nc.tensor.transpose(x_turned[:, u, :], x_words[:, u * P : (u + 1) * P], ident[:])
-        x_grouped = keep.tile([P, M, PACK], BF16, align_bytes=64)
-        nc.vector.tensor_copy(out=x_grouped[:].bitcast(F32), in_=x_turned[:].rearrange("q u m -> q m u"))
 
         w_in_words = w_in_sb[:].bitcast(F32)
         w_in_grouped = keep.tile([P, PACK, P, PACK], BF16, align_bytes=64)
@@ -124,40 +124,24 @@ def tile_brainquantumlayer_pa_s_kernel(
             w_in_turned = turned.tile([P, 2, P], F32, tag="turned")
             for u in range(2):
                 nc.tensor.transpose(w_in_turned[:, u, :], w_in_words[:, t, u * P : (u + 1) * P], ident[:])
-            empty = nc.scalar.copy if t % 2 == 0 else nc.vector.tensor_copy
-            empty(out=w_in_grouped[:, t].bitcast(F32), in_=w_in_turned[:].rearrange("q u j -> q j u"))
+            nc.scalar.copy(out=w_in_grouped[:, t].bitcast(F32), in_=w_in_turned[:].rearrange("q u j -> q j u"))
             if t == 0:
                 quantise(nc, x_mx, slice(0, M), x_grouped[:].rearrange("q m w -> q (m w)"))
-            else:
-                quantise(
-                    nc, w_in_mx, slice((t - 1) * P, t * P), w_in_grouped[:, t - 1].rearrange("q j w -> q (j w)")
-                )
-        t_spread = turned.tile([P, PACK, P], F32, tag="turned")
-        for t in range(PACK):
-            nc.tensor.transpose(t_spread[:, t, :], t4[:, t : t + 1].to_broadcast([P, P]), ident[:])
-        quantise(nc, w_in_mx, slice(3 * P, 4 * P), w_in_grouped[:, 3].rearrange("q j w -> q (j w)"))
+            quantise(nc, w_in_mx, slice(t * P, (t + 1) * P), w_in_grouped[:, t].rearrange("q j w -> q (j w)"))
+        sine = keep.tile([P, PACK], F32)
+        nc.scalar.activation(out=sine[:], in_=rest[:], func=ACT.Sin, scale=2.0)
+        t4 = keep.tile([P, PACK], F32)
+        nc.scalar.activation(out=t4[:], in_=sine[:], func=ACT.Abs, scale=0.1)
 
         state_ps = sums.tile([P, PACK, M], F32)
         for t in range(PACK):
             multiply_mx(nc, state_ps[:, t, :], w_in_mx, slice(t * P, (t + 1) * P), x_mx, slice(0, M))
-        noise_term = keep.tile([P, N], F32)
-        nc.vector.tensor_tensor(
-            out=noise_term[:].rearrange("m (j t) -> m j t", t=PACK),
-            in0=noise_sb[:].rearrange("m (j t) -> m j t", t=PACK),
-            in1=t_spread[:].rearrange("m t j -> m j t"),
-            op=ALU.mult,
-        )
-        state_f = keep.tile([P, M, PACK], F32)
-        nc.vector.tensor_tensor(
-            out=state_f[:],
-            in0=state_ps[:].rearrange("j t m -> j m t"),
-            in1=b_sb[:].unsqueeze(1).to_broadcast([P, M, PACK]),
-            op=ALU.add,
-        )
-        s_grouped = keep.tile([P, M, PACK], BF16, align_bytes=64)
-        nc.scalar.activation(out=s_grouped[:], in_=state_f[:], func=ACT.Tanh)
+        t_spread = turned.tile([P, PACK, P], F32, tag="turned")
+        for t in range(PACK):
+            nc.tensor.transpose(t_spread[:, t, :], t4[:, t : t + 1].to_broadcast([P, P]), ident[:])
         s_turned = keep.tile([P, PACK, M], F32)
-        nc.scalar.activation(out=s_turned[:], in_=state_f[:].rearrange("j m t -> j t m"), func=ACT.Tanh)
+        for t in range(PACK):
+            nc.scalar.activation(out=s_turned[:, t, :], in_=state_ps[:, t, :], func=ACT.Tanh, bias=b_sb[:, t : t + 1])
 
         raw = {"j": j_sb, "w": weights_sb}
         masked = {}
@@ -168,10 +152,9 @@ def tile_brainquantumlayer_pa_s_kernel(
             grouped[label] = keep.tile([P, N, PACK], BF16, name="grouped_" + label, align_bytes=64)
             mx[label] = mx_operand(keep, N, label)
 
-        def apply_mask(label, h):
-            cols = HALVES[h]
+        def apply_mask(label, rows):
             nc.vector.tensor_tensor(
-                out=masked[label][:, :, cols], in0=raw[label][:, :, cols], in1=mask_sb[:, :, cols], op=ALU.mult
+                out=masked[label][:, rows, :], in0=raw[label][:, rows, :], in1=mask_sb[:, rows, :], op=ALU.mult
             )
 
         def regroup(copy, label, h):
@@ -190,9 +173,11 @@ def tile_brainquantumlayer_pa_s_kernel(
         delta_ps = sums.tile([P, N], F32)
         signal_ps = sums.tile([P, N], F32)
 
-        apply_mask("j", 0)
+        for rows in ROW_HALVES:
+            apply_mask("j", rows)
         regroup(nc.scalar.copy, "j", 0)
-        apply_mask("j", 1)
+        s_grouped = keep.tile([P, M, PACK], BF16, align_bytes=64)
+        nc.vector.tensor_copy(out=s_grouped[:], in_=s_turned[:].rearrange("j t m -> j m t"))
         quantise(nc, s_mx, slice(0, M), s_grouped[:].rearrange("j m t -> j (m t)"))
         s_back = turned.tile([P, PACK, P], F32, tag="turned")
         for t in range(PACK):
@@ -202,26 +187,39 @@ def tile_brainquantumlayer_pa_s_kernel(
         nc.scalar.copy(
             out=s_sb[:].rearrange("m (j t) -> m j t", t=PACK), in_=s_back[:].rearrange("m t j -> m j t")
         )
-        apply_mask("w", 0)
+        for rows in ROW_HALVES:
+            apply_mask("w", rows)
         regroup(nc.scalar.copy, "w", 0)
-        apply_mask("w", 1)
+        regroup(nc.scalar.copy, "w", 1)
         state_grouped = keep.tile([P, M, PACK], BF16, align_bytes=64)
-        nc.scalar.copy(out=state_grouped[:], in_=state_f[:])
+        nc.vector.tensor_tensor(
+            out=state_grouped[:],
+            in0=state_ps[:].rearrange("j t m -> j m t"),
+            in1=b_sb[:].unsqueeze(1).to_broadcast([P, M, PACK]),
+            op=ALU.add,
+        )
         for h in range(2):
             quantise_masked("j", h)
             multiply_mx(nc, delta_ps[:, HALVES[h]], s_mx, slice(0, M), mx["j"], HALVES[h])
-        regroup(nc.vector.tensor_copy, "w", 1)
+        quantise(nc, state_mx, slice(0, M), state_grouped[:].rearrange("j m t -> j (m t)"))
+        noise_term = keep.tile([P, N], F32)
+        nc.vector.tensor_tensor(
+            out=noise_term[:].rearrange("m (j t) -> m j t", t=PACK),
+            in0=noise_sb[:].rearrange("m (j t) -> m j t", t=PACK),
+            in1=t_spread[:].rearrange("m t j -> m j t"),
+            op=ALU.mult,
+        )
+        quantise_masked("w", 0)
         delta = keep.tile([P, N], F32)
         nc.vector.scalar_tensor_tensor(
             out=delta[:], in0=delta_ps[:], scalar=lam_sb[:, 0:1], in1=s_sb[:], op0=ALU.mult, op1=ALU.mult
         )
-        quantise_masked("w", 0)
-        quantise(nc, state_mx, slice(0, M), state_grouped[:].rearrange("j m t -> j (m t)"))
         multiply_mx(nc, signal_ps[:, HALVES[0]], state_mx, slice(0, M), mx["w"], HALVES[0])
         quantise_masked("w", 1)
         multiply_mx(nc, signal_ps[:, HALVES[1]], state_mx, slice(0, M), mx["w"], HALVES[1])
         rest_of_sum = keep.tile([P, N], F32)
-        nc.vector.tensor_tensor(out=rest_of_sum[:], in0=delta[:], in1=noise_term[:], op=ALU.add)
+        for cols in HALVES:
+            nc.vector.tensor_tensor(out=rest_of_sum[:, cols], in0=delta[:, cols], in1=noise_term[:, cols], op=ALU.add)
 
         total = keep.tile([P, N], F32)
         out_sb = keep.tile([P, N], F32)

@@ -20,6 +20,7 @@ DI = 512
 N = 512
 HALF = N // 2
 HALVES = (slice(0, HALF), slice(HALF, N))
+ALL = slice(None)
 ROW_HALVES = (slice(0, 2), slice(2, PACK))
 
 FLOPS = 2 * M * N * (DI + N + N)
@@ -76,6 +77,8 @@ def tile_brainquantumlayer_pa_s_kernel(
         w_in_rows = W_in.rearrange("(p t) k -> p t k", t=PACK)
         for rows in ROW_HALVES:
             nc.sync.dma_start(out=w_in_sb[:, rows, :], in_=w_in_rows[:, rows, :])
+        noise_sb = keep.tile([P, N], BF16)
+        nc.sync.dma_start(out=noise_sb[:], in_=noise_raw)
         mask_sb = keep.tile([P, PACK, N], BF16)
         mask_rows = mask.rearrange("(p t) n -> p t n", t=PACK)
         j_sb = keep.tile([P, PACK, N], BF16)
@@ -85,11 +88,11 @@ def tile_brainquantumlayer_pa_s_kernel(
             nc.sync.dma_start(out=j_sb[:, rows, :], in_=j_rows[:, rows, :])
         weights_sb = keep.tile([P, PACK, N], BF16)
         nc.sync.dma_start(out=weights_sb[:], in_=weights.rearrange("(p t) n -> p t n", t=PACK))
-        noise_sb = keep.tile([P, N], BF16)
-        nc.sync.dma_start(out=noise_sb[:], in_=noise_raw)
 
         ident = keep.tile([P, P], F32)
         make_identity(nc, ident[:])
+        ident_bf = keep.tile([P, P], BF16)
+        nc.gpsimd.tensor_copy(out=ident_bf[:], in_=ident[:])
 
         zero = keep.tile([P, 1], F32)
         nc.vector.memset(zero[:], 0.0)
@@ -105,18 +108,11 @@ def tile_brainquantumlayer_pa_s_kernel(
         x_grouped = keep.tile([P, M, PACK], BF16, align_bytes=64)
         nc.vector.tensor_copy(out=x_grouped[:].bitcast(F32), in_=x_turned[:].rearrange("q u m -> q m u"))
 
-        turns_i = keep.tile([P, PACK], I32)
-        nc.vector.tensor_scalar(out=turns_i[:], in0=theta_sb[:], scalar1=2.0 / math.pi, scalar2=None, op0=ALU.mult)
-        turns = keep.tile([P, PACK], F32)
-        nc.vector.tensor_copy(out=turns[:], in_=turns_i[:])
+        turns = keep.tile([P, PACK], I32)
         rest_a = keep.tile([P, PACK], F32)
-        nc.vector.scalar_tensor_tensor(
-            out=rest_a[:], in0=turns[:], scalar=-HALF_PI_HEAD, in1=theta_sb[:], op0=ALU.mult, op1=ALU.add
-        )
         rest = keep.tile([P, PACK], F32)
-        nc.vector.scalar_tensor_tensor(
-            out=rest[:], in0=turns[:], scalar=-HALF_PI_TAIL, in1=rest_a[:], op0=ALU.mult, op1=ALU.add
-        )
+        sine = keep.tile([P, PACK], F32)
+        t4 = keep.tile([P, PACK], F32)
 
         w_in_words = w_in_sb[:].bitcast(F32)
         w_in_grouped = keep.tile([P, PACK, P, PACK], BF16, align_bytes=64)
@@ -126,19 +122,34 @@ def tile_brainquantumlayer_pa_s_kernel(
                 nc.tensor.transpose(w_in_turned[:, u, :], w_in_words[:, t, u * P : (u + 1) * P], ident[:])
             nc.scalar.copy(out=w_in_grouped[:, t].bitcast(F32), in_=w_in_turned[:].rearrange("q u j -> q j u"))
             if t == 0:
+                nc.vector.tensor_scalar(
+                    out=turns[:], in0=theta_sb[:], scalar1=2.0 / math.pi, scalar2=None, op0=ALU.mult
+                )
                 quantise(nc, x_mx, slice(0, M), x_grouped[:].rearrange("q m w -> q (m w)"))
+                nc.vector.scalar_tensor_tensor(
+                    out=rest_a[:], in0=turns[:], scalar=-HALF_PI_HEAD, in1=theta_sb[:], op0=ALU.mult, op1=ALU.add
+                )
+            if t == 1:
+                nc.vector.scalar_tensor_tensor(
+                    out=rest[:], in0=turns[:], scalar=-HALF_PI_TAIL, in1=rest_a[:], op0=ALU.mult, op1=ALU.add
+                )
+            if t == 2:
+                nc.scalar.activation(out=sine[:], in_=rest[:], func=ACT.Sin, scale=2.0)
+            if t == 3:
+                nc.scalar.activation(out=t4[:], in_=sine[:], func=ACT.Abs, scale=0.1)
             quantise(nc, w_in_mx, slice(t * P, (t + 1) * P), w_in_grouped[:, t].rearrange("q j w -> q (j w)"))
-        sine = keep.tile([P, PACK], F32)
-        nc.scalar.activation(out=sine[:], in_=rest[:], func=ACT.Sin, scale=2.0)
-        t4 = keep.tile([P, PACK], F32)
-        nc.scalar.activation(out=t4[:], in_=sine[:], func=ACT.Abs, scale=0.1)
+        noise_back = turned.tile([P, PACK, M], BF16, tag="turned")
+        for t in range(PACK):
+            nc.tensor.transpose(noise_back[:, t, :], noise_sb[:, t::PACK], ident_bf[:])
+        noise_scaled = keep.tile([P, PACK, M], F32)
+        for t in range(PACK):
+            nc.scalar.activation(
+                out=noise_scaled[:, t, :], in_=noise_back[:, t, :], func=ACT.Copy, scale=t4[:, t : t + 1]
+            )
 
         state_ps = sums.tile([P, PACK, M], F32)
         for t in range(PACK):
             multiply_mx(nc, state_ps[:, t, :], w_in_mx, slice(t * P, (t + 1) * P), x_mx, slice(0, M))
-        t_spread = turned.tile([P, PACK, P], F32, tag="turned")
-        for t in range(PACK):
-            nc.tensor.transpose(t_spread[:, t, :], t4[:, t : t + 1].to_broadcast([P, P]), ident[:])
         s_turned = keep.tile([P, PACK, M], F32)
         for t in range(PACK):
             nc.scalar.activation(out=s_turned[:, t, :], in_=state_ps[:, t, :], func=ACT.Tanh, bias=b_sb[:, t : t + 1])
@@ -152,9 +163,12 @@ def tile_brainquantumlayer_pa_s_kernel(
             grouped[label] = keep.tile([P, N, PACK], BF16, name="grouped_" + label, align_bytes=64)
             mx[label] = mx_operand(keep, N, label)
 
-        def apply_mask(label, rows):
+        def apply_mask(label, rows, cols):
             nc.vector.tensor_tensor(
-                out=masked[label][:, rows, :], in0=raw[label][:, rows, :], in1=mask_sb[:, rows, :], op=ALU.mult
+                out=masked[label][:, rows, cols],
+                in0=raw[label][:, rows, cols],
+                in1=mask_sb[:, rows, cols],
+                op=ALU.mult,
             )
 
         def regroup(copy, label, h):
@@ -174,23 +188,20 @@ def tile_brainquantumlayer_pa_s_kernel(
         signal_ps = sums.tile([P, N], F32)
 
         for rows in ROW_HALVES:
-            apply_mask("j", rows)
-        regroup(nc.scalar.copy, "j", 0)
+            apply_mask("j", rows, ALL)
         s_grouped = keep.tile([P, M, PACK], BF16, align_bytes=64)
-        nc.vector.tensor_copy(out=s_grouped[:], in_=s_turned[:].rearrange("j t m -> j m t"))
-        quantise(nc, s_mx, slice(0, M), s_grouped[:].rearrange("j m t -> j (m t)"))
+        nc.scalar.copy(out=s_grouped[:], in_=s_turned[:].rearrange("j t m -> j m t"))
+        regroup(nc.scalar.copy, "j", 0)
+        regroup(nc.vector.tensor_copy, "j", 1)
+        apply_mask("w", ALL, HALVES[0])
+        regroup(nc.scalar.copy, "w", 0)
+        apply_mask("w", ALL, HALVES[1])
+        noise_term = turned.tile([P, PACK, P], F32, tag="turned")
+        for t in range(PACK):
+            nc.tensor.transpose(noise_term[:, t, :], noise_scaled[:, t, :], ident[:])
         s_back = turned.tile([P, PACK, P], F32, tag="turned")
         for t in range(PACK):
             nc.tensor.transpose(s_back[:, t, :], s_turned[:, t, :], ident[:])
-        regroup(nc.vector.tensor_copy, "j", 1)
-        s_sb = keep.tile([P, N], F32)
-        nc.scalar.copy(
-            out=s_sb[:].rearrange("m (j t) -> m j t", t=PACK), in_=s_back[:].rearrange("m t j -> m j t")
-        )
-        for rows in ROW_HALVES:
-            apply_mask("w", rows)
-        regroup(nc.scalar.copy, "w", 0)
-        regroup(nc.scalar.copy, "w", 1)
         state_grouped = keep.tile([P, M, PACK], BF16, align_bytes=64)
         nc.vector.tensor_tensor(
             out=state_grouped[:],
@@ -198,17 +209,16 @@ def tile_brainquantumlayer_pa_s_kernel(
             in1=b_sb[:].unsqueeze(1).to_broadcast([P, M, PACK]),
             op=ALU.add,
         )
+        quantise(nc, s_mx, slice(0, M), s_grouped[:].rearrange("j m t -> j (m t)"))
+        s_sb = keep.tile([P, N], F32)
+        nc.scalar.copy(
+            out=s_sb[:].rearrange("m (j t) -> m j t", t=PACK), in_=s_back[:].rearrange("m t j -> m j t")
+        )
+        regroup(nc.scalar.copy, "w", 1)
         for h in range(2):
             quantise_masked("j", h)
             multiply_mx(nc, delta_ps[:, HALVES[h]], s_mx, slice(0, M), mx["j"], HALVES[h])
         quantise(nc, state_mx, slice(0, M), state_grouped[:].rearrange("j m t -> j (m t)"))
-        noise_term = keep.tile([P, N], F32)
-        nc.vector.tensor_tensor(
-            out=noise_term[:].rearrange("m (j t) -> m j t", t=PACK),
-            in0=noise_sb[:].rearrange("m (j t) -> m j t", t=PACK),
-            in1=t_spread[:].rearrange("m t j -> m j t"),
-            op=ALU.mult,
-        )
         quantise_masked("w", 0)
         delta = keep.tile([P, N], F32)
         nc.vector.scalar_tensor_tensor(
@@ -218,8 +228,13 @@ def tile_brainquantumlayer_pa_s_kernel(
         quantise_masked("w", 1)
         multiply_mx(nc, signal_ps[:, HALVES[1]], state_mx, slice(0, M), mx["w"], HALVES[1])
         rest_of_sum = keep.tile([P, N], F32)
-        for cols in HALVES:
-            nc.vector.tensor_tensor(out=rest_of_sum[:, cols], in0=delta[:, cols], in1=noise_term[:, cols], op=ALU.add)
+        for cols, js in zip(HALVES, (slice(0, P // 2), slice(P // 2, P))):
+            nc.vector.tensor_tensor(
+                out=rest_of_sum[:, cols].rearrange("m (j t) -> m j t", t=PACK),
+                in0=delta[:, cols].rearrange("m (j t) -> m j t", t=PACK),
+                in1=noise_term[:, :, js].rearrange("m t j -> m j t"),
+                op=ALU.add,
+            )
 
         total = keep.tile([P, N], F32)
         out_sb = keep.tile([P, N], F32)

@@ -68,8 +68,6 @@ def tile_brainquantumlayer_pa_s_kernel(
         nc.scalar.dma_start(out=theta_sb[:], in_=theta.rearrange("(p t) -> p t", t=PACK))
         b_sb = keep.tile([P, PACK], BF16)
         nc.scalar.dma_start(out=b_sb[:], in_=b_in.rearrange("(p t) -> p t", t=PACK))
-        lam_sb = keep.tile([P, 1], BF16)
-        nc.scalar.dma_start(out=lam_sb[:], in_=lam.partition_broadcast(P))
 
         x_sb = keep.tile([P, DI], BF16)
         nc.sync.dma_start(out=x_sb[:], in_=x)
@@ -88,6 +86,8 @@ def tile_brainquantumlayer_pa_s_kernel(
             nc.sync.dma_start(out=j_sb[:, rows, :], in_=j_rows[:, rows, :])
         weights_sb = keep.tile([P, PACK, N], BF16)
         nc.sync.dma_start(out=weights_sb[:], in_=weights.rearrange("(p t) n -> p t n", t=PACK))
+        lam_sb = keep.tile([P, 1], BF16)
+        nc.sync.dma_start(out=lam_sb[:], in_=lam.partition_broadcast(P))
 
         ident = keep.tile([P, P], F32)
         make_identity(nc, ident[:])

@@ -20,6 +20,7 @@ DI = 512
 N = 512
 HALF = N // 2
 HALVES = (slice(0, HALF), slice(HALF, N))
+PIECES = (slice(0, HALF), slice(HALF, HALF + P), slice(HALF + P, N))
 ALL = slice(None)
 ROW_HALVES = (slice(0, 2), slice(2, PACK))
 
@@ -147,7 +148,7 @@ def tile_brainquantumlayer_pa_s_kernel(
                 out=noise_scaled[:, t, :], in_=noise_back[:, t, :], func=ACT.Copy, scale=t4[:, t : t + 1]
             )
 
-        state_ps = sums.tile([P, PACK, M], F32)
+        state_ps = sums.tile([P, PACK, M], F32, tag="sums_a")
         for t in range(PACK):
             multiply_mx(nc, state_ps[:, t, :], w_in_mx, slice(t * P, (t + 1) * P), x_mx, slice(0, M))
         s_turned = keep.tile([P, PACK, M], F32)
@@ -171,30 +172,31 @@ def tile_brainquantumlayer_pa_s_kernel(
                 op=ALU.mult,
             )
 
-        def regroup(copy, label, h):
-            cols = HALVES[h]
+        def regroup(copy, label, cols):
             copy(
                 out=grouped[label][:, cols, :].rearrange("p (c i) t -> p c t i", i=4),
                 in_=masked[label][:, :, cols].rearrange("p t (c i) -> p c t i", i=4),
             )
 
-        def quantise_masked(label, h):
-            cols = HALVES[h]
+        def quantise_masked(label, cols):
             quantise(nc, mx[label], cols, grouped[label][:, cols, :].rearrange("p n t -> p (n t)"))
+
+        def multiply_signal(piece):
+            cols = PIECES[piece]
+            multiply_mx(nc, signal_ps[piece][:, cols], state_mx, slice(0, M), mx["w"], cols)
 
         s_mx = mx_operand(keep, M, "s")
         state_mx = mx_operand(keep, M, "state")
-        delta_ps = sums.tile([P, N], F32)
-        signal_ps = sums.tile([P, N], F32)
+        delta_ps = sums.tile([P, N], F32, tag="sums_b")
 
         for rows in ROW_HALVES:
             apply_mask("j", rows, ALL)
         s_grouped = keep.tile([P, M, PACK], BF16, align_bytes=64)
         nc.scalar.copy(out=s_grouped[:], in_=s_turned[:].rearrange("j t m -> j m t"))
-        regroup(nc.scalar.copy, "j", 0)
-        regroup(nc.vector.tensor_copy, "j", 1)
+        regroup(nc.scalar.copy, "j", HALVES[0])
+        regroup(nc.vector.tensor_copy, "j", HALVES[1])
         apply_mask("w", ALL, HALVES[0])
-        regroup(nc.scalar.copy, "w", 0)
+        regroup(nc.scalar.copy, "w", HALVES[0])
         apply_mask("w", ALL, HALVES[1])
         noise_term = turned.tile([P, PACK, P], F32, tag="turned")
         for t in range(PACK):
@@ -214,19 +216,23 @@ def tile_brainquantumlayer_pa_s_kernel(
         nc.scalar.copy(
             out=s_sb[:].rearrange("m (j t) -> m j t", t=PACK), in_=s_back[:].rearrange("m t j -> m j t")
         )
-        regroup(nc.scalar.copy, "w", 1)
-        for h in range(2):
-            quantise_masked("j", h)
-            multiply_mx(nc, delta_ps[:, HALVES[h]], s_mx, slice(0, M), mx["j"], HALVES[h])
+        for cols in PIECES[1:]:
+            regroup(nc.scalar.copy, "w", cols)
+        for cols in HALVES:
+            quantise_masked("j", cols)
+            multiply_mx(nc, delta_ps[:, cols], s_mx, slice(0, M), mx["j"], cols)
         quantise(nc, state_mx, slice(0, M), state_grouped[:].rearrange("j m t -> j (m t)"))
-        quantise_masked("w", 0)
+        quantise_masked("w", HALVES[0])
         delta = keep.tile([P, N], F32)
         nc.vector.scalar_tensor_tensor(
             out=delta[:], in0=delta_ps[:], scalar=lam_sb[:, 0:1], in1=s_sb[:], op0=ALU.mult, op1=ALU.mult
         )
-        multiply_mx(nc, signal_ps[:, HALVES[0]], state_mx, slice(0, M), mx["w"], HALVES[0])
-        quantise_masked("w", 1)
-        multiply_mx(nc, signal_ps[:, HALVES[1]], state_mx, slice(0, M), mx["w"], HALVES[1])
+        signal_ps = []
+        for piece, bank in enumerate(("sums_a", "sums_c", "sums_b")):
+            signal_ps.append(sums.tile([P, N], F32, name="signal_%d" % piece, tag=bank))
+        multiply_signal(0)
+        quantise_masked("w", PIECES[1])
+        multiply_signal(1)
         rest_of_sum = keep.tile([P, N], F32)
         for cols, js in zip(HALVES, (slice(0, P // 2), slice(P // 2, P))):
             nc.vector.tensor_tensor(
@@ -236,9 +242,14 @@ def tile_brainquantumlayer_pa_s_kernel(
                 op=ALU.add,
             )
 
+        quantise_masked("w", PIECES[2])
+        multiply_signal(2)
+
         total = keep.tile([P, N], F32)
         out_sb = keep.tile([P, N], F32)
-        for cols in HALVES:
-            nc.vector.tensor_tensor(out=total[:, cols], in0=signal_ps[:, cols], in1=rest_of_sum[:, cols], op=ALU.add)
+        for piece, cols in enumerate(PIECES):
+            nc.vector.tensor_tensor(
+                out=total[:, cols], in0=signal_ps[piece][:, cols], in1=rest_of_sum[:, cols], op=ALU.add
+            )
             nc.scalar.activation(out=out_sb[:, cols], in_=total[:, cols], func=ACT.Tanh)
             nc.sync.dma_start(out=out[:, cols], in_=out_sb[:, cols])

@@ -70,6 +70,10 @@ def tile_brainquantumlayer_pa_s_kernel(
         b_sb = keep.tile([P, PACK], BF16)
         nc.scalar.dma_start(out=b_sb[:], in_=b_in.rearrange("(p t) -> p t", t=PACK))
 
+        lam_row = keep.tile([P, 2], BF16)
+        nc.vector.memset(lam_row[:], 0.0)
+        nc.scalar.dma_start(out=lam_row[0:1, 0:1], in_=lam.unsqueeze(0))
+
         x_sb = keep.tile([P, DI], BF16)
         nc.sync.dma_start(out=x_sb[:], in_=x)
         w_in_sb = keep.tile([P, PACK, DI], BF16)
@@ -87,8 +91,6 @@ def tile_brainquantumlayer_pa_s_kernel(
             nc.sync.dma_start(out=j_sb[:, rows, :], in_=j_rows[:, rows, :])
         weights_sb = keep.tile([P, PACK, N], BF16)
         nc.sync.dma_start(out=weights_sb[:], in_=weights.rearrange("(p t) n -> p t n", t=PACK))
-        lam_sb = keep.tile([P, 1], BF16)
-        nc.sync.dma_start(out=lam_sb[:], in_=lam.partition_broadcast(P))
 
         ident = keep.tile([P, P], F32)
         make_identity(nc, ident[:])
@@ -151,6 +153,10 @@ def tile_brainquantumlayer_pa_s_kernel(
         state_ps = sums.tile([P, PACK, M], F32, tag="sums_a")
         for t in range(PACK):
             multiply_mx(nc, state_ps[:, t, :], w_in_mx, slice(t * P, (t + 1) * P), x_mx, slice(0, M))
+        lam_ps = turned.tile([P, 2], F32, tag="turned")
+        nc.tensor.matmul(
+            lam_ps[:], lhsT=lam_row[:, 0:1].to_broadcast([P, P]), rhs=ident_bf[:, 0:2], start=True, stop=True
+        )
         s_turned = keep.tile([P, PACK, M], F32)
         for t in range(PACK):
             nc.scalar.activation(out=s_turned[:, t, :], in_=state_ps[:, t, :], func=ACT.Tanh, bias=b_sb[:, t : t + 1])
@@ -194,6 +200,8 @@ def tile_brainquantumlayer_pa_s_kernel(
         s_grouped = keep.tile([P, M, PACK], BF16, align_bytes=64)
         nc.scalar.copy(out=s_grouped[:], in_=s_turned[:].rearrange("j t m -> j m t"))
         regroup(nc.scalar.copy, "j", HALVES[0])
+        lam_sb = keep.tile([P, 1], F32)
+        nc.vector.tensor_copy(out=lam_sb[:], in_=lam_ps[:, 0:1])
         regroup(nc.vector.tensor_copy, "j", HALVES[1])
         apply_mask("w", ALL, HALVES[0])
         regroup(nc.scalar.copy, "w", HALVES[0])

@@ -184,6 +184,14 @@ def tile_brainquantumlayer_pa_s_kernel(
                 in_=masked[label][:, :, cols].rearrange("p t (c i) -> p c t i", i=4),
             )
 
+        def mask_and_regroup(label, cols):
+            nc.vector.tensor_tensor(
+                out=grouped[label][:, cols, :].rearrange("p (c i) t -> p c t i", i=4),
+                in0=raw[label][:, :, cols].rearrange("p t (c i) -> p c t i", i=4),
+                in1=mask_sb[:, :, cols].rearrange("p t (c i) -> p c t i", i=4),
+                op=ALU.mult,
+            )
+
         def quantise_masked(label, cols):
             quantise(nc, mx[label], cols, grouped[label][:, cols, :].rearrange("p n t -> p (n t)"))
 
@@ -196,15 +204,15 @@ def tile_brainquantumlayer_pa_s_kernel(
         delta_ps = sums.tile([P, N], F32, tag="sums_b")
 
         for rows in ROW_HALVES:
-            apply_mask("j", rows, ALL)
-        s_grouped = keep.tile([P, M, PACK], BF16, align_bytes=64)
-        nc.scalar.copy(out=s_grouped[:], in_=s_turned[:].rearrange("j t m -> j m t"))
+            apply_mask("j", rows, HALVES[0])
         regroup(nc.scalar.copy, "j", HALVES[0])
         lam_sb = keep.tile([P, 1], F32)
         nc.vector.tensor_copy(out=lam_sb[:], in_=lam_ps[:, 0:1])
-        regroup(nc.vector.tensor_copy, "j", HALVES[1])
+        mask_and_regroup("j", HALVES[1])
         apply_mask("w", ALL, HALVES[0])
         regroup(nc.scalar.copy, "w", HALVES[0])
+        s_grouped = keep.tile([P, M, PACK], BF16, align_bytes=64)
+        nc.vector.tensor_copy(out=s_grouped[:], in_=s_turned[:].rearrange("j t m -> j m t"))
         apply_mask("w", ALL, HALVES[1])
         noise_term = turned.tile([P, PACK, P], F32, tag="turned")
         for t in range(PACK):
@@ -212,6 +220,10 @@ def tile_brainquantumlayer_pa_s_kernel(
         s_back = turned.tile([P, PACK, P], F32, tag="turned")
         for t in range(PACK):
             nc.tensor.transpose(s_back[:, t, :], s_turned[:, t, :], ident[:])
+        quantise(nc, s_mx, slice(0, M), s_grouped[:].rearrange("j m t -> j (m t)"))
+        for cols in HALVES:
+            quantise_masked("j", cols)
+            multiply_mx(nc, delta_ps[:, cols], s_mx, slice(0, M), mx["j"], cols)
         state_grouped = keep.tile([P, M, PACK], BF16, align_bytes=64)
         nc.vector.tensor_tensor(
             out=state_grouped[:],
@@ -219,18 +231,14 @@ def tile_brainquantumlayer_pa_s_kernel(
             in1=b_sb[:].unsqueeze(1).to_broadcast([P, M, PACK]),
             op=ALU.add,
         )
-        quantise(nc, s_mx, slice(0, M), s_grouped[:].rearrange("j m t -> j (m t)"))
         s_sb = keep.tile([P, N], F32)
         nc.scalar.copy(
             out=s_sb[:].rearrange("m (j t) -> m j t", t=PACK), in_=s_back[:].rearrange("m t j -> m j t")
         )
         for cols in PIECES[1:]:
             regroup(nc.scalar.copy, "w", cols)
-        for cols in HALVES:
-            quantise_masked("j", cols)
-            multiply_mx(nc, delta_ps[:, cols], s_mx, slice(0, M), mx["j"], cols)
-        quantise(nc, state_mx, slice(0, M), state_grouped[:].rearrange("j m t -> j (m t)"))
         quantise_masked("w", HALVES[0])
+        quantise(nc, state_mx, slice(0, M), state_grouped[:].rearrange("j m t -> j (m t)"))
         delta = keep.tile([P, N], F32)
         nc.vector.scalar_tensor_tensor(
             out=delta[:], in0=delta_ps[:], scalar=lam_sb[:, 0:1], in1=s_sb[:], op0=ALU.mult, op1=ALU.mult

@@ -119,11 +119,16 @@ def tile_brainquantumlayer_pa_s_kernel(
 
         w_in_words = w_in_sb[:].bitcast(F32)
         w_in_grouped = keep.tile([P, PACK, P, PACK], BF16, align_bytes=64)
+
+        def quantise_w_in(t):
+            quantise(nc, w_in_mx, slice(t * P, (t + 1) * P), w_in_grouped[:, t].rearrange("q j w -> q (j w)"))
+
         for t in range(PACK):
             w_in_turned = turned.tile([P, 2, P], F32, tag="turned")
             for u in range(2):
                 nc.tensor.transpose(w_in_turned[:, u, :], w_in_words[:, t, u * P : (u + 1) * P], ident[:])
-            nc.scalar.copy(out=w_in_grouped[:, t].bitcast(F32), in_=w_in_turned[:].rearrange("q u j -> q j u"))
+            empty = nc.scalar.copy if t % 2 == 0 else nc.vector.tensor_copy
+            empty(out=w_in_grouped[:, t].bitcast(F32), in_=w_in_turned[:].rearrange("q u j -> q j u"))
             if t == 0:
                 nc.vector.tensor_scalar(
                     out=turns[:], in0=theta_sb[:], scalar1=2.0 / math.pi, scalar2=None, op0=ALU.mult
@@ -132,15 +137,16 @@ def tile_brainquantumlayer_pa_s_kernel(
                 nc.vector.scalar_tensor_tensor(
                     out=rest_a[:], in0=turns[:], scalar=-HALF_PI_HEAD, in1=theta_sb[:], op0=ALU.mult, op1=ALU.add
                 )
+            else:
+                quantise_w_in(t - 1)
             if t == 1:
                 nc.vector.scalar_tensor_tensor(
                     out=rest[:], in0=turns[:], scalar=-HALF_PI_TAIL, in1=rest_a[:], op0=ALU.mult, op1=ALU.add
                 )
             if t == 2:
                 nc.scalar.activation(out=sine[:], in_=rest[:], func=ACT.Sin, scale=2.0)
-            if t == 3:
-                nc.scalar.activation(out=t4[:], in_=sine[:], func=ACT.Abs, scale=0.1)
-            quantise(nc, w_in_mx, slice(t * P, (t + 1) * P), w_in_grouped[:, t].rearrange("q j w -> q (j w)"))
+        quantise_w_in(3)
+        nc.scalar.activation(out=t4[:], in_=sine[:], func=ACT.Abs, scale=0.1)
         noise_back = turned.tile([P, PACK, M], BF16, tag="turned")
         for t in range(PACK):
             nc.tensor.transpose(noise_back[:, t, :], noise_sb[:, t::PACK], ident_bf[:])
@@ -184,14 +190,6 @@ def tile_brainquantumlayer_pa_s_kernel(
                 in_=masked[label][:, :, cols].rearrange("p t (c i) -> p c t i", i=4),
             )
 
-        def mask_and_regroup(label, cols):
-            nc.vector.tensor_tensor(
-                out=grouped[label][:, cols, :].rearrange("p (c i) t -> p c t i", i=4),
-                in0=raw[label][:, :, cols].rearrange("p t (c i) -> p c t i", i=4),
-                in1=mask_sb[:, :, cols].rearrange("p t (c i) -> p c t i", i=4),
-                op=ALU.mult,
-            )
-
         def quantise_masked(label, cols):
             quantise(nc, mx[label], cols, grouped[label][:, cols, :].rearrange("p n t -> p (n t)"))
 
@@ -199,16 +197,27 @@ def tile_brainquantumlayer_pa_s_kernel(
             cols = PIECES[piece]
             multiply_mx(nc, signal_ps[piece][:, cols], state_mx, slice(0, M), mx["w"], cols)
 
+        def add_noise(h):
+            cols = HALVES[h]
+            js = slice(h * P // 2, (h + 1) * P // 2)
+            nc.vector.tensor_tensor(
+                out=rest_of_sum[:, cols].rearrange("m (j t) -> m j t", t=PACK),
+                in0=delta[:, cols].rearrange("m (j t) -> m j t", t=PACK),
+                in1=noise_term[:, :, js].rearrange("m t j -> m j t"),
+                op=ALU.add,
+            )
+
         s_mx = mx_operand(keep, M, "s")
         state_mx = mx_operand(keep, M, "state")
         delta_ps = sums.tile([P, N], F32, tag="sums_b")
 
-        for rows in ROW_HALVES:
-            apply_mask("j", rows, HALVES[0])
+        apply_mask("j", ROW_HALVES[0], ALL)
+        apply_mask("j", ROW_HALVES[1], HALVES[1])
+        apply_mask("j", ROW_HALVES[1], HALVES[0])
         regroup(nc.scalar.copy, "j", HALVES[0])
         lam_sb = keep.tile([P, 1], F32)
         nc.vector.tensor_copy(out=lam_sb[:], in_=lam_ps[:, 0:1])
-        mask_and_regroup("j", HALVES[1])
+        regroup(nc.vector.tensor_copy, "j", HALVES[1])
         apply_mask("w", ALL, HALVES[0])
         regroup(nc.scalar.copy, "w", HALVES[0])
         s_grouped = keep.tile([P, M, PACK], BF16, align_bytes=64)
@@ -250,16 +259,10 @@ def tile_brainquantumlayer_pa_s_kernel(
         quantise_masked("w", PIECES[1])
         multiply_signal(1)
         rest_of_sum = keep.tile([P, N], F32)
-        for cols, js in zip(HALVES, (slice(0, P // 2), slice(P // 2, P))):
-            nc.vector.tensor_tensor(
-                out=rest_of_sum[:, cols].rearrange("m (j t) -> m j t", t=PACK),
-                in0=delta[:, cols].rearrange("m (j t) -> m j t", t=PACK),
-                in1=noise_term[:, :, js].rearrange("m t j -> m j t"),
-                op=ALU.add,
-            )
-
+        add_noise(0)
         quantise_masked("w", PIECES[2])
         multiply_signal(2)
+        add_noise(1)
 
         total = keep.tile([P, N], F32)
         out_sb = keep.tile([P, N], F32)

@@ -102,20 +102,29 @@ def tile_brainquantumlayer_pa_s_kernel(
         table_warm = keep.tile([P, 1], F32)
         nc.scalar.activation(out=table_warm[:], in_=zero[:], func=ACT.Silu)
 
+        warm = turned.tile([P, 3 * P], F32, tag="turned")
+        nc.tensor.matmul(
+            warm[:],
+            lhsT=zero[:].to_broadcast([P, P]),
+            rhs=zero[:].to_broadcast([P, 3 * P]),
+            start=True,
+            stop=True,
+        )
+
         x_mx = mx_operand(keep, M, "x")
         w_in_mx = mx_operand(keep, N, "w_in")
         x_words = x_sb[:].bitcast(F32)
         x_turned = turned.tile([P, 2, M], F32, tag="turned")
         for u in range(2):
             nc.tensor.transpose(x_turned[:, u, :], x_words[:, u * P : (u + 1) * P], ident[:])
-        x_grouped = keep.tile([P, M, PACK], BF16, align_bytes=64)
-        nc.vector.tensor_copy(out=x_grouped[:].bitcast(F32), in_=x_turned[:].rearrange("q u m -> q m u"))
-
         turns = keep.tile([P, PACK], I32)
         rest_a = keep.tile([P, PACK], F32)
         rest = keep.tile([P, PACK], F32)
         sine = keep.tile([P, PACK], F32)
         t4 = keep.tile([P, PACK], F32)
+        nc.vector.tensor_scalar(out=turns[:], in0=theta_sb[:], scalar1=2.0 / math.pi, scalar2=None, op0=ALU.mult)
+        x_grouped = keep.tile([P, M, PACK], BF16, align_bytes=64)
+        nc.vector.tensor_copy(out=x_grouped[:].bitcast(F32), in_=x_turned[:].rearrange("q u m -> q m u"))
 
         w_in_words = w_in_sb[:].bitcast(F32)
         w_in_grouped = keep.tile([P, PACK, P, PACK], BF16, align_bytes=64)
@@ -130,23 +139,20 @@ def tile_brainquantumlayer_pa_s_kernel(
             empty = nc.scalar.copy if t % 2 == 0 else nc.vector.tensor_copy
             empty(out=w_in_grouped[:, t].bitcast(F32), in_=w_in_turned[:].rearrange("q u j -> q j u"))
             if t == 0:
-                nc.vector.tensor_scalar(
-                    out=turns[:], in0=theta_sb[:], scalar1=2.0 / math.pi, scalar2=None, op0=ALU.mult
+                nc.vector.scalar_tensor_tensor(
+                    out=rest_a[:], in0=turns[:], scalar=-HALF_PI_HEAD, in1=theta_sb[:], op0=ALU.mult, op1=ALU.add
                 )
                 quantise(nc, x_mx, slice(0, M), x_grouped[:].rearrange("q m w -> q (m w)"))
                 nc.vector.scalar_tensor_tensor(
-                    out=rest_a[:], in0=turns[:], scalar=-HALF_PI_HEAD, in1=theta_sb[:], op0=ALU.mult, op1=ALU.add
+                    out=rest[:], in0=turns[:], scalar=-HALF_PI_TAIL, in1=rest_a[:], op0=ALU.mult, op1=ALU.add
                 )
             else:
                 quantise_w_in(t - 1)
             if t == 1:
-                nc.vector.scalar_tensor_tensor(
-                    out=rest[:], in0=turns[:], scalar=-HALF_PI_TAIL, in1=rest_a[:], op0=ALU.mult, op1=ALU.add
-                )
-            if t == 2:
                 nc.scalar.activation(out=sine[:], in_=rest[:], func=ACT.Sin, scale=2.0)
+            if t == 2:
+                nc.scalar.activation(out=t4[:], in_=sine[:], func=ACT.Abs, scale=0.1)
         quantise_w_in(3)
-        nc.scalar.activation(out=t4[:], in_=sine[:], func=ACT.Abs, scale=0.1)
         noise_back = turned.tile([P, PACK, M], BF16, tag="turned")
         for t in range(PACK):
             nc.tensor.transpose(noise_back[:, t, :], noise_sb[:, t::PACK], ident_bf[:])

@@ -72,7 +72,6 @@ def tile_brainquantumlayer_pa_s_kernel(
 
         lam_row = keep.tile([P, 2], BF16)
         nc.vector.memset(lam_row[:], 0.0)
-        nc.scalar.dma_start(out=lam_row[0:1, 0:1], in_=lam.unsqueeze(0))
 
         x_sb = keep.tile([P, DI], BF16)
         nc.sync.dma_start(out=x_sb[:], in_=x)
@@ -83,14 +82,14 @@ def tile_brainquantumlayer_pa_s_kernel(
         noise_sb = keep.tile([P, N], BF16)
         nc.sync.dma_start(out=noise_sb[:], in_=noise_raw)
         mask_sb = keep.tile([P, PACK, N], BF16)
-        mask_rows = mask.rearrange("(p t) n -> p t n", t=PACK)
+        nc.sync.dma_start(out=mask_sb[:], in_=mask.rearrange("(p t) n -> p t n", t=PACK))
         j_sb = keep.tile([P, PACK, N], BF16)
         j_rows = J.rearrange("(p t) n -> p t n", t=PACK)
         for rows in ROW_HALVES:
-            nc.sync.dma_start(out=mask_sb[:, rows, :], in_=mask_rows[:, rows, :])
             nc.sync.dma_start(out=j_sb[:, rows, :], in_=j_rows[:, rows, :])
         weights_sb = keep.tile([P, PACK, N], BF16)
         nc.sync.dma_start(out=weights_sb[:], in_=weights.rearrange("(p t) n -> p t n", t=PACK))
+        nc.sync.dma_start(out=lam_row[0:1, 0:1], in_=lam.unsqueeze(0))
 
         ident = keep.tile([P, P], F32)
         make_identity(nc, ident[:])
@@ -165,10 +164,6 @@ def tile_brainquantumlayer_pa_s_kernel(
         state_ps = sums.tile([P, PACK, M], F32, tag="sums_a")
         for t in range(PACK):
             multiply_mx(nc, state_ps[:, t, :], w_in_mx, slice(t * P, (t + 1) * P), x_mx, slice(0, M))
-        lam_ps = turned.tile([P, 2], F32, tag="turned")
-        nc.tensor.matmul(
-            lam_ps[:], lhsT=lam_row[:, 0:1].to_broadcast([P, P]), rhs=ident_bf[:, 0:2], start=True, stop=True
-        )
         s_turned = keep.tile([P, PACK, M], F32)
         for t in range(PACK):
             nc.scalar.activation(out=s_turned[:, t, :], in_=state_ps[:, t, :], func=ACT.Tanh, bias=b_sb[:, t : t + 1])
@@ -221,8 +216,6 @@ def tile_brainquantumlayer_pa_s_kernel(
         apply_mask("j", ROW_HALVES[1], HALVES[1])
         apply_mask("j", ROW_HALVES[1], HALVES[0])
         regroup(nc.scalar.copy, "j", HALVES[0])
-        lam_sb = keep.tile([P, 1], F32)
-        nc.vector.tensor_copy(out=lam_sb[:], in_=lam_ps[:, 0:1])
         regroup(nc.vector.tensor_copy, "j", HALVES[1])
         apply_mask("w", ALL, HALVES[0])
         regroup(nc.scalar.copy, "w", HALVES[0])
@@ -235,6 +228,10 @@ def tile_brainquantumlayer_pa_s_kernel(
         s_back = turned.tile([P, PACK, P], F32, tag="turned")
         for t in range(PACK):
             nc.tensor.transpose(s_back[:, t, :], s_turned[:, t, :], ident[:])
+        lam_ps = turned.tile([P, 2], F32, tag="turned")
+        nc.tensor.matmul(
+            lam_ps[:], lhsT=lam_row[:, 0:1].to_broadcast([P, P]), rhs=ident_bf[:, 0:2], start=True, stop=True
+        )
         quantise(nc, s_mx, slice(0, M), s_grouped[:].rearrange("j m t -> j (m t)"))
         for cols in HALVES:
             quantise_masked("j", cols)
@@ -256,7 +253,7 @@ def tile_brainquantumlayer_pa_s_kernel(
         quantise(nc, state_mx, slice(0, M), state_grouped[:].rearrange("j m t -> j (m t)"))
         delta = keep.tile([P, N], F32)
         nc.vector.scalar_tensor_tensor(
-            out=delta[:], in0=delta_ps[:], scalar=lam_sb[:, 0:1], in1=s_sb[:], op0=ALU.mult, op1=ALU.mult
+            out=delta[:], in0=delta_ps[:], scalar=lam_ps[:, 0:1], in1=s_sb[:], op0=ALU.mult, op1=ALU.mult
         )
         signal_ps = []
         for piece, bank in enumerate(("sums_a", "sums_c", "sums_b")):

@@ -79,14 +79,15 @@ def tile_brainquantumlayer_pa_s_kernel(
         w_in_rows = W_in.rearrange("(p t) k -> p t k", t=PACK)
         for rows in ROW_HALVES:
             nc.sync.dma_start(out=w_in_sb[:, rows, :], in_=w_in_rows[:, rows, :])
-        noise_sb = keep.tile([P, N], BF16)
-        nc.sync.dma_start(out=noise_sb[:], in_=noise_raw)
         mask_sb = keep.tile([P, PACK, N], BF16)
-        nc.sync.dma_start(out=mask_sb[:], in_=mask.rearrange("(p t) n -> p t n", t=PACK))
+        mask_rows = mask.rearrange("(p t) n -> p t n", t=PACK)
         j_sb = keep.tile([P, PACK, N], BF16)
         j_rows = J.rearrange("(p t) n -> p t n", t=PACK)
         for rows in ROW_HALVES:
+            nc.sync.dma_start(out=mask_sb[:, rows, :], in_=mask_rows[:, rows, :])
             nc.sync.dma_start(out=j_sb[:, rows, :], in_=j_rows[:, rows, :])
+        noise_sb = keep.tile([P, N], BF16)
+        nc.sync.dma_start(out=noise_sb[:], in_=noise_raw)
         weights_sb = keep.tile([P, PACK, N], BF16)
         nc.sync.dma_start(out=weights_sb[:], in_=weights.rearrange("(p t) n -> p t n", t=PACK))
         nc.sync.dma_start(out=lam_row[0:1, 0:1], in_=lam.unsqueeze(0))
@@ -152,14 +153,6 @@ def tile_brainquantumlayer_pa_s_kernel(
             if t == 2:
                 nc.scalar.activation(out=t4[:], in_=sine[:], func=ACT.Abs, scale=0.1)
         quantise_w_in(3)
-        noise_back = turned.tile([P, PACK, M], BF16, tag="turned")
-        for t in range(PACK):
-            nc.tensor.transpose(noise_back[:, t, :], noise_sb[:, t::PACK], ident_bf[:])
-        noise_scaled = keep.tile([P, PACK, M], F32)
-        for t in range(PACK):
-            nc.scalar.activation(
-                out=noise_scaled[:, t, :], in_=noise_back[:, t, :], func=ACT.Copy, scale=t4[:, t : t + 1]
-            )
 
         state_ps = sums.tile([P, PACK, M], F32, tag="sums_a")
         for t in range(PACK):
@@ -213,29 +206,43 @@ def tile_brainquantumlayer_pa_s_kernel(
         delta_ps = sums.tile([P, N], F32, tag="sums_b")
 
         apply_mask("j", ROW_HALVES[0], ALL)
-        apply_mask("j", ROW_HALVES[1], HALVES[1])
         apply_mask("j", ROW_HALVES[1], HALVES[0])
         regroup(nc.scalar.copy, "j", HALVES[0])
-        regroup(nc.vector.tensor_copy, "j", HALVES[1])
-        apply_mask("w", ALL, HALVES[0])
-        regroup(nc.scalar.copy, "w", HALVES[0])
+        apply_mask("j", ROW_HALVES[1], HALVES[1])
         s_grouped = keep.tile([P, M, PACK], BF16, align_bytes=64)
         nc.vector.tensor_copy(out=s_grouped[:], in_=s_turned[:].rearrange("j t m -> j m t"))
-        apply_mask("w", ALL, HALVES[1])
-        noise_term = turned.tile([P, PACK, P], F32, tag="turned")
+        regroup(nc.vector.tensor_copy, "j", HALVES[1])
+        noise_back = turned.tile([P, PACK, M], BF16, tag="turned")
         for t in range(PACK):
-            nc.tensor.transpose(noise_term[:, t, :], noise_scaled[:, t, :], ident[:])
+            nc.tensor.transpose(noise_back[:, t, :], noise_sb[:, t::PACK], ident_bf[:])
+        noise_scaled = keep.tile([P, PACK, M], F32)
+        for t in range(PACK):
+            nc.scalar.activation(
+                out=noise_scaled[:, t, :], in_=noise_back[:, t, :], func=ACT.Copy, scale=t4[:, t : t + 1]
+            )
         s_back = turned.tile([P, PACK, P], F32, tag="turned")
         for t in range(PACK):
             nc.tensor.transpose(s_back[:, t, :], s_turned[:, t, :], ident[:])
+        s_sb = keep.tile([P, N], F32)
+        nc.scalar.copy(
+            out=s_sb[:].rearrange("m (j t) -> m j t", t=PACK), in_=s_back[:].rearrange("m t j -> m j t")
+        )
+        apply_mask("w", ALL, HALVES[0])
+        regroup(nc.scalar.copy, "w", HALVES[0])
+        quantise(nc, s_mx, slice(0, M), s_grouped[:].rearrange("j m t -> j (m t)"))
         lam_ps = turned.tile([P, 2], F32, tag="turned")
         nc.tensor.matmul(
             lam_ps[:], lhsT=lam_row[:, 0:1].to_broadcast([P, P]), rhs=ident_bf[:, 0:2], start=True, stop=True
         )
-        quantise(nc, s_mx, slice(0, M), s_grouped[:].rearrange("j m t -> j (m t)"))
-        for cols in HALVES:
+        noise_term = turned.tile([P, PACK, P], F32, tag="turned")
+        for t in range(PACK):
+            nc.tensor.transpose(noise_term[:, t, :], noise_scaled[:, t, :], ident[:])
+        for cols in reversed(HALVES):
             quantise_masked("j", cols)
             multiply_mx(nc, delta_ps[:, cols], s_mx, slice(0, M), mx["j"], cols)
+        apply_mask("w", ALL, HALVES[1])
+        for cols in PIECES[1:]:
+            regroup(nc.scalar.copy, "w", cols)
         state_grouped = keep.tile([P, M, PACK], BF16, align_bytes=64)
         nc.vector.tensor_tensor(
             out=state_grouped[:],
@@ -243,29 +250,23 @@ def tile_brainquantumlayer_pa_s_kernel(
             in1=b_sb[:].unsqueeze(1).to_broadcast([P, M, PACK]),
             op=ALU.add,
         )
-        s_sb = keep.tile([P, N], F32)
-        nc.scalar.copy(
-            out=s_sb[:].rearrange("m (j t) -> m j t", t=PACK), in_=s_back[:].rearrange("m t j -> m j t")
-        )
-        for cols in PIECES[1:]:
-            regroup(nc.scalar.copy, "w", cols)
-        quantise_masked("w", HALVES[0])
-        quantise(nc, state_mx, slice(0, M), state_grouped[:].rearrange("j m t -> j (m t)"))
         delta = keep.tile([P, N], F32)
         nc.vector.scalar_tensor_tensor(
             out=delta[:], in0=delta_ps[:], scalar=lam_ps[:, 0:1], in1=s_sb[:], op0=ALU.mult, op1=ALU.mult
         )
+        quantise(nc, state_mx, slice(0, M), state_grouped[:].rearrange("j m t -> j (m t)"))
+        quantise_masked("w", HALVES[0])
         signal_ps = []
         for piece, bank in enumerate(("sums_a", "sums_c", "sums_b")):
             signal_ps.append(sums.tile([P, N], F32, name="signal_%d" % piece, tag=bank))
         multiply_signal(0)
-        quantise_masked("w", PIECES[1])
-        multiply_signal(1)
         rest_of_sum = keep.tile([P, N], F32)
         add_noise(0)
+        quantise_masked("w", PIECES[1])
+        multiply_signal(1)
+        add_noise(1)
         quantise_masked("w", PIECES[2])
         multiply_signal(2)
-        add_noise(1)
 
         total = keep.tile([P, N], F32)
         out_sb = keep.tile([P, N], F32)

@@ -65,11 +65,6 @@ def tile_brainquantumlayer_pa_s_kernel(
         sums = ctx.enter_context(tc.psum_pool(name="sums", bufs=1))
         ctx.enter_context(tc.manual_schedule())
 
-        theta_sb = keep.tile([P, PACK], BF16)
-        nc.scalar.dma_start(out=theta_sb[:], in_=theta.rearrange("(p t) -> p t", t=PACK))
-        b_sb = keep.tile([P, PACK], BF16)
-        nc.scalar.dma_start(out=b_sb[:], in_=b_in.rearrange("(p t) -> p t", t=PACK))
-
         lam_row = keep.tile([P, 2], BF16)
         nc.vector.memset(lam_row[:], 0.0)
 
@@ -79,6 +74,10 @@ def tile_brainquantumlayer_pa_s_kernel(
         w_in_rows = W_in.rearrange("(p t) k -> p t k", t=PACK)
         for rows in ROW_HALVES:
             nc.sync.dma_start(out=w_in_sb[:, rows, :], in_=w_in_rows[:, rows, :])
+        theta_sb = keep.tile([P, PACK], BF16)
+        nc.sync.dma_start(out=theta_sb[:], in_=theta.rearrange("(p t) -> p t", t=PACK))
+        b_sb = keep.tile([P, PACK], BF16)
+        nc.sync.dma_start(out=b_sb[:], in_=b_in.rearrange("(p t) -> p t", t=PACK))
         mask_sb = keep.tile([P, PACK, N], BF16)
         mask_rows = mask.rearrange("(p t) n -> p t n", t=PACK)
         j_sb = keep.tile([P, PACK, N], BF16)
@@ -122,7 +121,6 @@ def tile_brainquantumlayer_pa_s_kernel(
         rest = keep.tile([P, PACK], F32)
         sine = keep.tile([P, PACK], F32)
         t4 = keep.tile([P, PACK], F32)
-        nc.vector.tensor_scalar(out=turns[:], in0=theta_sb[:], scalar1=2.0 / math.pi, scalar2=None, op0=ALU.mult)
         x_grouped = keep.tile([P, M, PACK], BF16, align_bytes=64)
         nc.vector.tensor_copy(out=x_grouped[:].bitcast(F32), in_=x_turned[:].rearrange("q u m -> q m u"))
 
@@ -139,20 +137,23 @@ def tile_brainquantumlayer_pa_s_kernel(
             empty = nc.scalar.copy if t % 2 == 0 else nc.vector.tensor_copy
             empty(out=w_in_grouped[:, t].bitcast(F32), in_=w_in_turned[:].rearrange("q u j -> q j u"))
             if t == 0:
+                quantise(nc, x_mx, slice(0, M), x_grouped[:].rearrange("q m w -> q (m w)"))
+            if t == 1:
+                nc.vector.tensor_scalar(
+                    out=turns[:], in0=theta_sb[:], scalar1=2.0 / math.pi, scalar2=None, op0=ALU.mult
+                )
+            if t == 3:
                 nc.vector.scalar_tensor_tensor(
                     out=rest_a[:], in0=turns[:], scalar=-HALF_PI_HEAD, in1=theta_sb[:], op0=ALU.mult, op1=ALU.add
                 )
-                quantise(nc, x_mx, slice(0, M), x_grouped[:].rearrange("q m w -> q (m w)"))
-                nc.vector.scalar_tensor_tensor(
-                    out=rest[:], in0=turns[:], scalar=-HALF_PI_TAIL, in1=rest_a[:], op0=ALU.mult, op1=ALU.add
-                )
-            else:
+            if t > 0:
                 quantise_w_in(t - 1)
-            if t == 1:
-                nc.scalar.activation(out=sine[:], in_=rest[:], func=ACT.Sin, scale=2.0)
-            if t == 2:
-                nc.scalar.activation(out=t4[:], in_=sine[:], func=ACT.Abs, scale=0.1)
         quantise_w_in(3)
+        nc.vector.scalar_tensor_tensor(
+            out=rest[:], in0=turns[:], scalar=-HALF_PI_TAIL, in1=rest_a[:], op0=ALU.mult, op1=ALU.add
+        )
+        nc.scalar.activation(out=sine[:], in_=rest[:], func=ACT.Sin, scale=2.0)
+        nc.scalar.activation(out=t4[:], in_=sine[:], func=ACT.Abs, scale=0.1)
 
         state_ps = sums.tile([P, PACK, M], F32, tag="sums_a")
         for t in range(PACK):

@@ -26,9 +26,6 @@ ROW_HALVES = (slice(0, 2), slice(2, PACK))
 
 FLOPS = 2 * M * N * (DI + N + N)
 
-HALF_PI_HEAD = 1.5703125
-HALF_PI_TAIL = math.pi / 2 - HALF_PI_HEAD
-
 
 def quantise(nc, operand, cols, grouped):
     nc.vector.quantize_mx(
@@ -117,7 +114,6 @@ def tile_brainquantumlayer_pa_s_kernel(
         for u in range(2):
             nc.tensor.transpose(x_turned[:, u, :], x_words[:, u * P : (u + 1) * P], ident[:])
         turns = keep.tile([P, PACK], I32)
-        rest_a = keep.tile([P, PACK], F32)
         rest = keep.tile([P, PACK], F32)
         sine = keep.tile([P, PACK], F32)
         t4 = keep.tile([P, PACK], F32)
@@ -134,7 +130,7 @@ def tile_brainquantumlayer_pa_s_kernel(
             w_in_turned = turned.tile([P, 2, P], F32, tag="turned")
             for u in range(2):
                 nc.tensor.transpose(w_in_turned[:, u, :], w_in_words[:, t, u * P : (u + 1) * P], ident[:])
-            empty = nc.scalar.copy if t % 2 == 0 else nc.vector.tensor_copy
+            empty = nc.vector.tensor_copy if t == 1 else nc.scalar.copy
             empty(out=w_in_grouped[:, t].bitcast(F32), in_=w_in_turned[:].rearrange("q u j -> q j u"))
             if t == 0:
                 quantise(nc, x_mx, slice(0, M), x_grouped[:].rearrange("q m w -> q (m w)"))
@@ -144,15 +140,12 @@ def tile_brainquantumlayer_pa_s_kernel(
                 )
             if t == 3:
                 nc.vector.scalar_tensor_tensor(
-                    out=rest_a[:], in0=turns[:], scalar=-HALF_PI_HEAD, in1=theta_sb[:], op0=ALU.mult, op1=ALU.add
+                    out=rest[:], in0=turns[:], scalar=-math.pi / 2, in1=theta_sb[:], op0=ALU.mult, op1=ALU.add
                 )
             if t > 0:
                 quantise_w_in(t - 1)
-        quantise_w_in(3)
-        nc.vector.scalar_tensor_tensor(
-            out=rest[:], in0=turns[:], scalar=-HALF_PI_TAIL, in1=rest_a[:], op0=ALU.mult, op1=ALU.add
-        )
         nc.scalar.activation(out=sine[:], in_=rest[:], func=ACT.Sin, scale=2.0)
+        quantise_w_in(3)
         nc.scalar.activation(out=t4[:], in_=sine[:], func=ACT.Abs, scale=0.1)
 
         state_ps = sums.tile([P, PACK, M], F32, tag="sums_a")
@@ -228,19 +221,19 @@ def tile_brainquantumlayer_pa_s_kernel(
         nc.scalar.copy(
             out=s_sb[:].rearrange("m (j t) -> m j t", t=PACK), in_=s_back[:].rearrange("m t j -> m j t")
         )
+        quantise(nc, s_mx, slice(0, M), s_grouped[:].rearrange("j m t -> j (m t)"))
         apply_mask("w", ALL, HALVES[0])
         regroup(nc.scalar.copy, "w", HALVES[0])
-        quantise(nc, s_mx, slice(0, M), s_grouped[:].rearrange("j m t -> j (m t)"))
         lam_ps = turned.tile([P, 2], F32, tag="turned")
         nc.tensor.matmul(
             lam_ps[:], lhsT=lam_row[:, 0:1].to_broadcast([P, P]), rhs=ident_bf[:, 0:2], start=True, stop=True
         )
-        noise_term = turned.tile([P, PACK, P], F32, tag="turned")
-        for t in range(PACK):
-            nc.tensor.transpose(noise_term[:, t, :], noise_scaled[:, t, :], ident[:])
         for cols in reversed(HALVES):
             quantise_masked("j", cols)
             multiply_mx(nc, delta_ps[:, cols], s_mx, slice(0, M), mx["j"], cols)
+        noise_term = turned.tile([P, PACK, P], F32, tag="turned")
+        for t in range(PACK):
+            nc.tensor.transpose(noise_term[:, t, :], noise_scaled[:, t, :], ident[:])
         apply_mask("w", ALL, HALVES[1])
         for cols in PIECES[1:]:
             regroup(nc.scalar.copy, "w", cols)

@@ -20,7 +20,9 @@ DI = 512
 N = 512
 HALF = N // 2
 HALVES = (slice(0, HALF), slice(HALF, N))
-PIECES = (slice(0, HALF), slice(HALF, HALF + P), slice(HALF + P, N))
+PIECES = (slice(0, HALF), slice(HALF + P, N), slice(HALF, HALF + P))
+VECTOR_PART = slice(HALF, HALF + 3 * HALF // 4)
+SCALAR_PART = slice(HALF + 3 * HALF // 4, N)
 ALL = slice(None)
 ROW_HALVES = (slice(0, 2), slice(2, PACK))
 
@@ -148,12 +150,27 @@ def tile_brainquantumlayer_pa_s_kernel(
         quantise_w_in(3)
         nc.scalar.activation(out=t4[:], in_=sine[:], func=ACT.Abs, scale=0.1)
 
-        state_ps = sums.tile([P, PACK, M], F32, tag="sums_a")
+        state_halves = [
+            sums.tile([P, PACK // 2, M], F32, name="state_half_%d" % h, tag=bank)
+            for h, bank in enumerate(("sums_a", "sums_b"))
+        ]
+        state_ps = sums.tile([P, PACK, M], F32, tag="sums_c")
+
+        def multiply_state(acc, t):
+            multiply_mx(nc, acc, w_in_mx, slice(t * P, (t + 1) * P), x_mx, slice(0, M))
+
         for t in range(PACK):
-            multiply_mx(nc, state_ps[:, t, :], w_in_mx, slice(t * P, (t + 1) * P), x_mx, slice(0, M))
+            multiply_state(state_halves[t // 2][:, t % 2, :], t)
+        for t in range(PACK):
+            multiply_state(state_ps[:, t, :], t)
         s_turned = keep.tile([P, PACK, M], F32)
         for t in range(PACK):
-            nc.scalar.activation(out=s_turned[:, t, :], in_=state_ps[:, t, :], func=ACT.Tanh, bias=b_sb[:, t : t + 1])
+            nc.scalar.activation(
+                out=s_turned[:, t, :],
+                in_=state_halves[t // 2][:, t % 2, :],
+                func=ACT.Tanh,
+                bias=b_sb[:, t : t + 1],
+            )
 
         raw = {"j": j_sb, "w": weights_sb}
         masked = {}
@@ -200,12 +217,13 @@ def tile_brainquantumlayer_pa_s_kernel(
         delta_ps = sums.tile([P, N], F32, tag="sums_b")
 
         apply_mask("j", ROW_HALVES[0], ALL)
+        apply_mask("j", ROW_HALVES[1], HALVES[1])
+        regroup(nc.scalar.copy, "j", SCALAR_PART)
         apply_mask("j", ROW_HALVES[1], HALVES[0])
         regroup(nc.scalar.copy, "j", HALVES[0])
-        apply_mask("j", ROW_HALVES[1], HALVES[1])
+        regroup(nc.vector.tensor_copy, "j", VECTOR_PART)
         s_grouped = keep.tile([P, M, PACK], BF16, align_bytes=64)
         nc.vector.tensor_copy(out=s_grouped[:], in_=s_turned[:].rearrange("j t m -> j m t"))
-        regroup(nc.vector.tensor_copy, "j", HALVES[1])
         noise_back = turned.tile([P, PACK, M], BF16, tag="turned")
         for t in range(PACK):
             nc.tensor.transpose(noise_back[:, t, :], noise_sb[:, t::PACK], ident_bf[:])
@@ -221,6 +239,7 @@ def tile_brainquantumlayer_pa_s_kernel(
         nc.scalar.copy(
             out=s_sb[:].rearrange("m (j t) -> m j t", t=PACK), in_=s_back[:].rearrange("m t j -> m j t")
         )
+        quantise_masked("j", HALVES[1])
         quantise(nc, s_mx, slice(0, M), s_grouped[:].rearrange("j m t -> j (m t)"))
         apply_mask("w", ALL, HALVES[0])
         regroup(nc.scalar.copy, "w", HALVES[0])
@@ -228,15 +247,22 @@ def tile_brainquantumlayer_pa_s_kernel(
         nc.tensor.matmul(
             lam_ps[:], lhsT=lam_row[:, 0:1].to_broadcast([P, P]), rhs=ident_bf[:, 0:2], start=True, stop=True
         )
+        quantise_masked("j", HALVES[0])
         for cols in reversed(HALVES):
-            quantise_masked("j", cols)
             multiply_mx(nc, delta_ps[:, cols], s_mx, slice(0, M), mx["j"], cols)
         noise_term = turned.tile([P, PACK, P], F32, tag="turned")
         for t in range(PACK):
             nc.tensor.transpose(noise_term[:, t, :], noise_scaled[:, t, :], ident[:])
         apply_mask("w", ALL, HALVES[1])
-        for cols in PIECES[1:]:
-            regroup(nc.scalar.copy, "w", cols)
+        regroup(nc.scalar.copy, "w", PIECES[2])
+        nc.gpsimd.tensor_scalar(
+            out=grouped["w"][:, PIECES[1], :],
+            in0=masked["w"][:, :, PIECES[1]].rearrange("p t c -> p c t"),
+            scalar1=1.0,
+            scalar2=0.0,
+            op0=ALU.mult,
+            op1=ALU.add,
+        )
         state_grouped = keep.tile([P, M, PACK], BF16, align_bytes=64)
         nc.vector.tensor_tensor(
             out=state_grouped[:],
@@ -254,13 +280,13 @@ def tile_brainquantumlayer_pa_s_kernel(
         for piece, bank in enumerate(("sums_a", "sums_c", "sums_b")):
             signal_ps.append(sums.tile([P, N], F32, name="signal_%d" % piece, tag=bank))
         multiply_signal(0)
-        rest_of_sum = keep.tile([P, N], F32)
-        add_noise(0)
         quantise_masked("w", PIECES[1])
         multiply_signal(1)
-        add_noise(1)
+        rest_of_sum = keep.tile([P, N], F32)
+        add_noise(0)
         quantise_masked("w", PIECES[2])
         multiply_signal(2)
+        add_noise(1)
 
         total = keep.tile([P, N], F32)
         out_sb = keep.tile([P, N], F32)

from contextlib import ExitStack
import math

import concourse.mybir as mybir
from concourse.masks import make_identity

F32 = mybir.dt.float32
BF16 = mybir.dt.bfloat16
I32 = mybir.dt.int32
U32 = mybir.dt.uint32
U8 = mybir.dt.uint8
FP8X4 = mybir.dt.float8_e4m3fn_x4
ALU = mybir.AluOpType
ACT = mybir.ActivationFunctionType

P = 128
PACK = 4
M = 128
DI = 512
N = 512
HALF = N // 2
HALVES = (slice(0, HALF), slice(HALF, N))
PIECES = (slice(0, HALF), slice(HALF + P, N), slice(HALF, HALF + P))
VECTOR_PART = slice(HALF, HALF + 3 * HALF // 4)
SCALAR_PART = slice(HALF + 3 * HALF // 4, N)
ALL = slice(None)
ROW_HALVES = (slice(0, 2), slice(2, PACK))

FLOPS = 2 * M * N * (DI + N + N)


def quantise(nc, operand, cols, grouped):
    nc.vector.quantize_mx(
        out=operand["codes"][:, cols].bitcast(FP8X4), scales=operand["scales"][:, cols], in_=grouped
    )


def mx_operand(pool, width, label):
    return {
        "codes": pool.tile([P, width], U32, name="codes_" + label, align_bytes=64),
        "scales": pool.tile([P, width], U8, name="scales_" + label, align_bytes=64),
    }


def multiply_mx(nc, acc, stationary, s_cols, moving, m_cols):
    nc.tensor.matmul_mx(
        out=acc,
        lhsT=stationary["codes"][:, s_cols].bitcast(FP8X4),
        lhsT_scale=stationary["scales"][:, s_cols],
        rhs=moving["codes"][:, m_cols].bitcast(FP8X4),
        rhs_scale=moving["scales"][:, m_cols],
        start=True,
        stop=True,
    )


def tile_brainquantumlayer_pa_s_kernel(
    tc, x, W_in, b_in, weights, J, theta, lam, mask, noise_raw, out
):
    nc = tc.nc
    with ExitStack() as ctx:
        keep = ctx.enter_context(tc.tile_pool(name="keep", bufs=1))
        turned = ctx.enter_context(tc.psum_pool(name="turned", bufs=5))
        sums = ctx.enter_context(tc.psum_pool(name="sums", bufs=1))
        ctx.enter_context(tc.manual_schedule())

        lam_row = keep.tile([P, 2], BF16)
        nc.vector.memset(lam_row[:], 0.0)

        x_sb = keep.tile([P, DI], BF16)
        nc.sync.dma_start(out=x_sb[:], in_=x)
        w_in_sb = keep.tile([P, PACK, DI], BF16)
        w_in_rows = W_in.rearrange("(p t) k -> p t k", t=PACK)
        for rows in ROW_HALVES:
            nc.sync.dma_start(out=w_in_sb[:, rows, :], in_=w_in_rows[:, rows, :])
        theta_sb = keep.tile([P, PACK], BF16)
        nc.sync.dma_start(out=theta_sb[:], in_=theta.rearrange("(p t) -> p t", t=PACK))
        b_sb = keep.tile([P, PACK], BF16)
        nc.sync.dma_start(out=b_sb[:], in_=b_in.rearrange("(p t) -> p t", t=PACK))
        mask_sb = keep.tile([P, PACK, N], BF16)
        mask_rows = mask.rearrange("(p t) n -> p t n", t=PACK)
        j_sb = keep.tile([P, PACK, N], BF16)
        j_rows = J.rearrange("(p t) n -> p t n", t=PACK)
        for rows in ROW_HALVES:
            nc.sync.dma_start(out=mask_sb[:, rows, :], in_=mask_rows[:, rows, :])
            nc.sync.dma_start(out=j_sb[:, rows, :], in_=j_rows[:, rows, :])
        noise_sb = keep.tile([P, N], BF16)
        nc.sync.dma_start(out=noise_sb[:], in_=noise_raw)
        weights_sb = keep.tile([P, PACK, N], BF16)
        nc.sync.dma_start(out=weights_sb[:], in_=weights.rearrange("(p t) n -> p t n", t=PACK))
        nc.sync.dma_start(out=lam_row[0:1, 0:1], in_=lam.unsqueeze(0))

        ident = keep.tile([P, P], F32)
        make_identity(nc, ident[:])
        ident_bf = keep.tile([P, P], BF16)
        nc.gpsimd.tensor_copy(out=ident_bf[:], in_=ident[:])

        zero = keep.tile([P, 1], F32)
        nc.vector.memset(zero[:], 0.0)
        table_warm = keep.tile([P, 1], F32)
        nc.scalar.activation(out=table_warm[:], in_=zero[:], func=ACT.Silu)

        warm = turned.tile([P, 3 * P], F32, tag="turned")
        nc.tensor.matmul(
            warm[:],
            lhsT=zero[:].to_broadcast([P, P]),
            rhs=zero[:].to_broadcast([P, 3 * P]),
            start=True,
            stop=True,
        )

        x_mx = mx_operand(keep, M, "x")
        w_in_mx = mx_operand(keep, N, "w_in")
        x_words = x_sb[:].bitcast(F32)
        x_turned = turned.tile([P, 2, M], F32, tag="turned")
        for u in range(2):
            nc.tensor.transpose(x_turned[:, u, :], x_words[:, u * P : (u + 1) * P], ident[:])
        turns = keep.tile([P, PACK], I32)
        rest = keep.tile([P, PACK], F32)
        sine = keep.tile([P, PACK], F32)
        t4 = keep.tile([P, PACK], F32)
        x_grouped = keep.tile([P, M, PACK], BF16, align_bytes=64)
        nc.vector.tensor_copy(out=x_grouped[:].bitcast(F32), in_=x_turned[:].rearrange("q u m -> q m u"))

        w_in_words = w_in_sb[:].bitcast(F32)
        w_in_grouped = keep.tile([P, PACK, P, PACK], BF16, align_bytes=64)

        def quantise_w_in(t):
            quantise(nc, w_in_mx, slice(t * P, (t + 1) * P), w_in_grouped[:, t].rearrange("q j w -> q (j w)"))

        for t in range(PACK):
            w_in_turned = turned.tile([P, 2, P], F32, tag="turned")
            for u in range(2):
                nc.tensor.transpose(w_in_turned[:, u, :], w_in_words[:, t, u * P : (u + 1) * P], ident[:])
            empty = nc.vector.tensor_copy if t == 1 else nc.scalar.copy
            empty(out=w_in_grouped[:, t].bitcast(F32), in_=w_in_turned[:].rearrange("q u j -> q j u"))
            if t == 0:
                quantise(nc, x_mx, slice(0, M), x_grouped[:].rearrange("q m w -> q (m w)"))
            if t == 1:
                nc.vector.tensor_scalar(
                    out=turns[:], in0=theta_sb[:], scalar1=2.0 / math.pi, scalar2=None, op0=ALU.mult
                )
            if t == 3:
                nc.vector.scalar_tensor_tensor(
                    out=rest[:], in0=turns[:], scalar=-math.pi / 2, in1=theta_sb[:], op0=ALU.mult, op1=ALU.add
                )
            if t > 0:
                quantise_w_in(t - 1)
        nc.scalar.activation(out=sine[:], in_=rest[:], func=ACT.Sin, scale=2.0)
        quantise_w_in(3)
        nc.scalar.activation(out=t4[:], in_=sine[:], func=ACT.Abs, scale=0.1)

        state_halves = [
            sums.tile([P, PACK // 2, M], F32, name="state_half_%d" % h, tag=bank)
            for h, bank in enumerate(("sums_a", "sums_b"))
        ]
        state_ps = sums.tile([P, PACK, M], F32, tag="sums_c")

        def multiply_state(acc, t):
            multiply_mx(nc, acc, w_in_mx, slice(t * P, (t + 1) * P), x_mx, slice(0, M))

        for t in range(PACK):
            multiply_state(state_halves[t // 2][:, t % 2, :], t)
        for t in range(PACK):
            multiply_state(state_ps[:, t, :], t)
        s_turned = keep.tile([P, PACK, M], F32)
        for t in range(PACK):
            nc.scalar.activation(
                out=s_turned[:, t, :],
                in_=state_halves[t // 2][:, t % 2, :],
                func=ACT.Tanh,
                bias=b_sb[:, t : t + 1],
            )

        raw = {"j": j_sb, "w": weights_sb}
        masked = {}
        grouped = {}
        mx = {}
        for label in ("j", "w"):
            masked[label] = keep.tile([P, PACK, N], BF16, name="masked_" + label)
            grouped[label] = keep.tile([P, N, PACK], BF16, name="grouped_" + label, align_bytes=64)
            mx[label] = mx_operand(keep, N, label)

        def apply_mask(label, rows, cols):
            nc.vector.tensor_tensor(
                out=masked[label][:, rows, cols],
                in0=raw[label][:, rows, cols],
                in1=mask_sb[:, rows, cols],
                op=ALU.mult,
            )

        def regroup(copy, label, cols):
            copy(
                out=grouped[label][:, cols, :].rearrange("p (c i) t -> p c t i", i=4),
                in_=masked[label][:, :, cols].rearrange("p t (c i) -> p c t i", i=4),
            )

        def quantise_masked(label, cols):
            quantise(nc, mx[label], cols, grouped[label][:, cols, :].rearrange("p n t -> p (n t)"))

        def multiply_signal(piece):
            cols = PIECES[piece]
            multiply_mx(nc, signal_ps[piece][:, cols], state_mx, slice(0, M), mx["w"], cols)

        def add_noise(h):
            cols = HALVES[h]
            js = slice(h * P // 2, (h + 1) * P // 2)
            nc.vector.tensor_tensor(
                out=rest_of_sum[:, cols].rearrange("m (j t) -> m j t", t=PACK),
                in0=delta[:, cols].rearrange("m (j t) -> m j t", t=PACK),
                in1=noise_term[:, :, js].rearrange("m t j -> m j t"),
                op=ALU.add,
            )

        s_mx = mx_operand(keep, M, "s")
        state_mx = mx_operand(keep, M, "state")
        delta_ps = sums.tile([P, N], F32, tag="sums_b")

        apply_mask("j", ROW_HALVES[0], ALL)
        apply_mask("j", ROW_HALVES[1], HALVES[1])
        regroup(nc.scalar.copy, "j", SCALAR_PART)
        apply_mask("j", ROW_HALVES[1], HALVES[0])
        regroup(nc.scalar.copy, "j", HALVES[0])
        regroup(nc.vector.tensor_copy, "j", VECTOR_PART)
        s_grouped = keep.tile([P, M, PACK], BF16, align_bytes=64)
        nc.vector.tensor_copy(out=s_grouped[:], in_=s_turned[:].rearrange("j t m -> j m t"))
        noise_back = turned.tile([P, PACK, M], BF16, tag="turned")
        for t in range(PACK):
            nc.tensor.transpose(noise_back[:, t, :], noise_sb[:, t::PACK], ident_bf[:])
        noise_scaled = keep.tile([P, PACK, M], F32)
        for t in range(PACK):
            nc.scalar.activation(
                out=noise_scaled[:, t, :], in_=noise_back[:, t, :], func=ACT.Copy, scale=t4[:, t : t + 1]
            )
        s_back = turned.tile([P, PACK, P], F32, tag="turned")
        for t in range(PACK):
            nc.tensor.transpose(s_back[:, t, :], s_turned[:, t, :], ident[:])
        s_sb = keep.tile([P, N], F32)
        nc.scalar.copy(
            out=s_sb[:].rearrange("m (j t) -> m j t", t=PACK), in_=s_back[:].rearrange("m t j -> m j t")
        )
        quantise_masked("j", HALVES[1])
        quantise(nc, s_mx, slice(0, M), s_grouped[:].rearrange("j m t -> j (m t)"))
        apply_mask("w", ALL, HALVES[0])
        regroup(nc.scalar.copy, "w", HALVES[0])
        lam_ps = turned.tile([P, 2], F32, tag="turned")
        nc.tensor.matmul(
            lam_ps[:], lhsT=lam_row[:, 0:1].to_broadcast([P, P]), rhs=ident_bf[:, 0:2], start=True, stop=True
        )
        quantise_masked("j", HALVES[0])
        for cols in reversed(HALVES):
            multiply_mx(nc, delta_ps[:, cols], s_mx, slice(0, M), mx["j"], cols)
        noise_term = turned.tile([P, PACK, P], F32, tag="turned")
        for t in range(PACK):
            nc.tensor.transpose(noise_term[:, t, :], noise_scaled[:, t, :], ident[:])
        apply_mask("w", ALL, HALVES[1])
        regroup(nc.scalar.copy, "w", PIECES[2])
        nc.gpsimd.tensor_scalar(
            out=grouped["w"][:, PIECES[1], :],
            in0=masked["w"][:, :, PIECES[1]].rearrange("p t c -> p c t"),
            scalar1=1.0,
            scalar2=0.0,
            op0=ALU.mult,
            op1=ALU.add,
        )
        state_grouped = keep.tile([P, M, PACK], BF16, align_bytes=64)
        nc.vector.tensor_tensor(
            out=state_grouped[:],
            in0=state_ps[:].rearrange("j t m -> j m t"),
            in1=b_sb[:].unsqueeze(1).to_broadcast([P, M, PACK]),
            op=ALU.add,
        )
        delta = keep.tile([P, N], F32)
        nc.vector.scalar_tensor_tensor(
            out=delta[:], in0=delta_ps[:], scalar=lam_ps[:, 0:1], in1=s_sb[:], op0=ALU.mult, op1=ALU.mult
        )
        quantise(nc, state_mx, slice(0, M), state_grouped[:].rearrange("j m t -> j (m t)"))
        quantise_masked("w", HALVES[0])
        signal_ps = []
        for piece, bank in enumerate(("sums_a", "sums_c", "sums_b")):
            signal_ps.append(sums.tile([P, N], F32, name="signal_%d" % piece, tag=bank))
        multiply_signal(0)
        quantise_masked("w", PIECES[1])
        multiply_signal(1)
        rest_of_sum = keep.tile([P, N], F32)
        add_noise(0)
        quantise_masked("w", PIECES[2])
        multiply_signal(2)
        add_noise(1)

        total = keep.tile([P, N], F32)
        out_sb = keep.tile([P, N], F32)
        for piece, cols in enumerate(PIECES):
            nc.vector.tensor_tensor(
                out=total[:, cols], in0=signal_ps[piece][:, cols], in1=rest_of_sum[:, cols], op=ALU.add
            )
            nc.scalar.activation(out=out_sb[:, cols], in_=total[:, cols], func=ACT.Tanh)
            nc.sync.dma_start(out=out[:, cols], in_=out_sb[:, cols])
